import numpy as np
import ml_dtypes


def mxq(x, axis, fmt="e4m3"):
    dtype, down = {"e4m3": (ml_dtypes.float8_e4m3fn, 7), "e5m2": (ml_dtypes.float8_e5m2, 14)}[fmt]
    v = np.moveaxis(np.asarray(x, np.float32).astype(ml_dtypes.bfloat16).astype(np.float64), axis, -1)
    blocks = v.reshape(v.shape[:-1] + (-1, 32))
    amax = np.abs(blocks).max(-1, keepdims=True)
    byte = np.maximum(np.where(amax > 0, np.frexp(amax)[1] - 1 + 127, 0) - down, 1)
    scale = np.exp2(byte - 127.0)
    codes = (blocks / scale).astype(np.float32).astype(dtype).astype(np.float64)
    return np.moveaxis((codes * scale).reshape(v.shape), -1, axis)


WIDE = False


def mx_kscale(k):
    if not WIDE:
        return np.ones(k)
    levels = np.array([10, -10, 5, -5, 0])
    a = np.random.permutation(np.resize(levels, k // 512 * 4)).reshape(k // 512, 4)
    idx = np.arange(k)
    return np.exp2(a[idx // 512, idx % 128 // 32])


BF16 = ml_dtypes.bfloat16


def bf(x):
    return np.asarray(x, np.float32).astype(BF16)


def f64(x):
    return np.asarray(x).astype(np.float64)


E2M1 = np.array([0.0, 0.5, 1.0, 1.5, 2.0, 3.0, 4.0, 6.0, -0.0, -0.5, -1.0, -1.5, -2.0, -3.0, -4.0, -6.0])


def pack_weight(w, fmt):
    k, n = w.shape
    w = f64(bf(w)).reshape(k // 32, 32, n)
    amax = np.abs(w).max(1)
    if fmt == "e4m3":
        byte = np.frexp(amax)[1] - 1 + 127 - 7
    else:
        mant, ex = np.frexp(amax / 6.0)
        byte = np.where(mant > 0.5, ex, ex - 1) + 127
    byte = np.clip(np.where(amax > 0, byte, 1), 1, 254)
    scaled = (w * np.exp2(127.0 - byte)[:, None, :]).reshape(k, n).astype(np.float32)
    by_word = np.ascontiguousarray(scaled.reshape(k // 512, 128, 4, n).transpose(0, 1, 3, 2))
    if fmt == "e4m3":
        words = by_word.astype(ml_dtypes.float8_e4m3fn).view(np.uint8)
    else:
        c = by_word.astype(ml_dtypes.float4_e2m1fn).view(np.uint8) & 0xF
        words = c[..., 0::2] | (c[..., 1::2] << 4)
    return np.ascontiguousarray(words), np.ascontiguousarray(byte.astype(np.uint8).reshape(k // 512, 16, n))


def unpack_weight(words, scales, fmt):
    g, p, n, _ = words.shape
    if fmt == "e4m3":
        vals = np.ascontiguousarray(words).view(ml_dtypes.float8_e4m3fn).astype(np.float64)
    else:
        nib = np.empty((g, p, n, 4), np.uint8)
        nib[..., 0::2] = words & 0xF
        nib[..., 1::2] = words >> 4
        vals = E2M1[nib]
    vals = vals * np.repeat(np.exp2(scales.astype(np.float64) - 127.0), 8, axis=1)[..., None]
    return vals.transpose(0, 1, 3, 2).reshape(g * 512, n)

def pack4(w):
    words, scales = pack_weight(w, "e2m1")
    return words.reshape(words.shape[0], 128, -1), scales


def unpack4(words, scales):
    return unpack_weight(words.reshape(words.shape[0], 128, -1, 2), scales, "e2m1")


B, I, H = 1024, 1024, 1024
G = 2 * H
EPS = 1e-5


def ln(v):
    mu = v.mean(-1, keepdims=True)
    var = np.square(v - mu).mean(-1, keepdims=True)
    return (v - mu) / np.sqrt(var + EPS)


def sigmoid(v):
    return 1.0 / (1.0 + np.exp(-v))


def setup_inputs():
    s, t = mx_kscale(I), mx_kscale(H)
    x = bf(np.random.standard_normal((B, I)) * s)
    h = bf(np.random.standard_normal((B, H)) * t)
    irz_words, irz_scales = pack4((np.random.standard_normal((G, I)) / np.sqrt(I) / s).T)
    b_irz = bf(np.random.standard_normal(G) * 0.5)
    hrz_words, hrz_scales = pack4((np.random.standard_normal((G, H)) / np.sqrt(H) / t).T)
    b_hrz = bf(np.random.standard_normal(G) * 0.5)
    return {"x": x,
            "h": h,
            "W_irz_words": irz_words,
            "W_irz_scales": irz_scales,
            "b_irz": b_irz,
            "W_hrz_words": hrz_words,
            "W_hrz_scales": hrz_scales,
            "b_hrz": b_hrz}


def reference(x, h, W_irz_words, W_irz_scales, b_irz, W_hrz_words, W_hrz_scales, b_hrz):
    i_rz = ln((mxq(f64(x), 1, "e4m3") @ unpack4(W_irz_words, W_irz_scales)) + f64(b_irz))
    h_rz = ln((mxq(f64(h), 1, "e4m3") @ unpack4(W_hrz_words, W_hrz_scales)) + f64(b_hrz))
    return sigmoid(i_rz + h_rz)

@@ -1,0 +1,230 @@
+from contextlib import ExitStack
+
+import concourse.mybir as mybir
+from concourse.masks import make_identity
+
+F32 = mybir.dt.float32
+BF16 = mybir.dt.bfloat16
+I32 = mybir.dt.int32
+U32 = mybir.dt.uint32
+U8 = mybir.dt.uint8
+FP8X4 = mybir.dt.float8_e4m3fn_x4
+FP4X4 = mybir.dt.float4_e2m1fn_x4
+ALU = mybir.AluOpType
+ACT = mybir.ActivationFunctionType
+
+P = 128
+ROWS = 1024
+K = 1024
+GATES = 2048
+EPS = 1e-5
+BRANCHES = 2
+ROW_TILES = ROWS // P
+K_PASS = 4 * P
+PASSES = K // K_PASS
+BANK = 512
+BANKS = GATES // BANK
+HALVES = 2
+STORE_CHUNKS = 2
+
+FLOPS = 2 * BRANCHES * ROWS * K * GATES
+
+
+def tile_layernormgrucell_pa_kernel(
+    tc, x, h, W_irz_words, W_irz_scales, b_irz, W_hrz_words, W_hrz_scales, b_hrz, out
+):
+    nc = tc.nc
+    acts = (x, h)
+    weight_words = (W_irz_words, W_hrz_words)
+    weight_scales = (W_irz_scales, W_hrz_scales)
+    biases = (b_irz, b_hrz)
+
+    with ExitStack() as ctx:
+        keep = ctx.enter_context(tc.tile_pool(name="keep", bufs=1))
+        stage = ctx.enter_context(tc.tile_pool(name="stage", bufs=2))
+        small = ctx.enter_context(tc.tile_pool(name="small", bufs=3))
+        acc_pool = ctx.enter_context(tc.psum_pool(name="acc", bufs=6))
+        turn_pool = ctx.enter_context(tc.psum_pool(name="turn", bufs=2))
+        ctx.enter_context(tc.manual_schedule())
+
+        raw = keep.tile([P, BRANCHES, ROW_TILES, K], BF16)
+        w_words = keep.tile([P, BRANCHES, PASSES, 2 * GATES], U8, align_bytes=64)
+        w_planes = keep.tile([P, BRANCHES, PASSES, GATES], U8, align_bytes=64)
+        bias_all = keep.tile([P, BRANCHES, GATES], BF16)
+        ident = keep.tile([P, P], F32)
+        minus_half = keep.tile([P, BRANCHES], F32)
+        warm = keep.tile([P, 1], F32)
+
+        nc.vector.memset(w_planes[:].bitcast(I32), 0)
+        nc.vector.memset(minus_half[:], -0.5)
+        make_identity(nc, ident[:])
+        nc.scalar.activation(out=warm[:], in_=minus_half[:, 0:1], func=ACT.Sigmoid)
+
+        def load_rows(m):
+            for b in range(BRANCHES):
+                nc.sync.dma_start(out=raw[:, b, m, :], in_=acts[b][m * P : (m + 1) * P, :])
+
+        def load_scales(b):
+            planes = w_planes[:].bitcast(I32)
+            rows = weight_scales[b].bitcast(I32)
+            for q in range(8):
+                first = 32 * (q // 4) + q % 4
+                nc.sync.dma_start(
+                    out=planes[first : P : 64, b, :, :],
+                    in_=rows[:, q : 16 : 8, :].rearrange("g q c -> q g c"),
+                )
+
+        def load_words(b):
+            words = w_words[:].bitcast(I32)
+            source = weight_words[b].bitcast(I32)
+            step = 2 * BANK // 4
+            for n in range(BANKS):
+                nc.sync.dma_start(
+                    out=words[:, b, :, n * step : (n + 1) * step],
+                    in_=source[:, :, n * step : (n + 1) * step].rearrange("g p c -> p g c"),
+                )
+            nc.sync.dma_start(out=bias_all[:, b, :], in_=biases[b].partition_broadcast(P))
+
+        load_rows(0)
+        load_scales(0)
+        load_scales(1)
+        load_words(0)
+        load_rows(1)
+        load_words(1)
+        for m in range(2, ROW_TILES):
+            load_rows(m)
+
+        def turn(m):
+            grouped = []
+            for b in range(BRANCHES):
+                words = raw[:, b, m, :].bitcast(F32)
+                turned = turn_pool.tile([P, PASSES * HALVES, P], F32, name="turned")
+                for g in range(PASSES):
+                    for u in range(HALVES):
+                        first = g * K_PASS // 2 + u
+                        nc.tensor.transpose(
+                            turned[:, g * HALVES + u, :],
+                            words[:, first : (g + 1) * K_PASS // 2 : HALVES],
+                            ident[:],
+                        )
+                side = stage.tile([P, PASSES * P * 4], BF16, align_bytes=64, name="side%d" % b)
+                nc.scalar.copy(
+                    out=side[:].bitcast(F32).rearrange("p (g r u) -> p g r u", g=PASSES, u=HALVES),
+                    in_=turned[:].rearrange("p (g u) r -> p g r u", u=HALVES),
+                )
+                grouped.append(side)
+            return grouped
+
+        def quantise(grouped):
+            packed = []
+            for b in range(BRANCHES):
+                codes = stage.tile([P, PASSES * P], U32, align_bytes=64, name="codes%d" % b)
+                plane = stage.tile([P, PASSES * P], U8, align_bytes=64, name="plane%d" % b)
+                nc.vector.quantize_mx(
+                    out=codes[:].bitcast(FP8X4), scales=plane[:], in_=grouped[b][:]
+                )
+                packed.append((codes, plane))
+            return packed
+
+        def product(b, packed, v, sums):
+            codes, plane = packed[b]
+            for n in range(BANKS):
+                acc = acc_pool.tile([P, BANK], F32, name="acc")
+                for g in range(PASSES):
+                    nc.tensor.matmul_mx(
+                        out=acc[:],
+                        lhsT=codes[:, g * P : (g + 1) * P].bitcast(FP8X4),
+                        lhsT_scale=plane[:, g * P : (g + 1) * P],
+                        rhs=w_words[:, b, g, n * 2 * BANK : (n + 1) * 2 * BANK].bitcast(FP4X4),
+                        rhs_scale=w_planes[:, b, g, n * BANK : (n + 1) * BANK],
+                        start=(g == 0),
+                        stop=(g == PASSES - 1),
+                    )
+                cols = slice(n * BANK, (n + 1) * BANK)
+                nc.vector.scalar_tensor_tensor(
+                    out=v[:, b, cols],
+                    in0=acc[:],
+                    scalar=1.0,
+                    in1=bias_all[:, b, cols],
+                    op0=ALU.mult,
+                    op1=ALU.add,
+                    accum_out=sums[:, n : n + 1],
+                )
+
+        def spread(b, v, sums, neg_mean, sum_sq):
+            pair = small.tile([P, 2], F32, name="pair")
+            nc.gpsimd.tensor_tensor(out=pair[:], in0=sums[:, 0:2], in1=sums[:, 2:4], op=ALU.add)
+            nc.gpsimd.tensor_scalar(
+                out=neg_mean[:, b : b + 1],
+                in0=pair[:, 0:1],
+                scalar1=pair[:, 1:2],
+                scalar2=-1.0 / GATES,
+                op0=ALU.add,
+                op1=ALU.mult,
+            )
+            squares = stage.tile([P, GATES], BF16, name="squares")
+            nc.scalar.activation(
+                out=squares[:],
+                in_=v[:, b, :],
+                func=ACT.Square,
+                bias=neg_mean[:, b : b + 1],
+                scale=1.0,
+                accum_out=sum_sq[:, b : b + 1],
+            )
+
+        def row_factors(neg_mean, sum_sq):
+            var_eps = small.tile([P, BRANCHES], F32, name="var_eps")
+            rstd = small.tile([P, BRANCHES], F32, name="rstd")
+            parts = small.tile([P, BRANCHES], F32, name="parts")
+            shift = small.tile([P, 1], F32, name="shift")
+            ratio = small.tile([P, 1], F32, name="ratio")
+            nc.gpsimd.tensor_scalar(
+                out=var_eps[:], in0=sum_sq[:], scalar1=1.0 / GATES, scalar2=EPS,
+                op0=ALU.mult, op1=ALU.add,
+            )
+            nc.gpsimd.tensor_tensor(out=rstd[:], in0=var_eps[:], in1=minus_half[:], op=ALU.pow)
+            nc.gpsimd.tensor_tensor(out=parts[:], in0=rstd[:], in1=neg_mean[:], op=ALU.mult)
+            nc.gpsimd.tensor_tensor(out=shift[:], in0=parts[:, 0:1], in1=parts[:, 1:2], op=ALU.add)
+            nc.gpsimd.tensor_scalar(
+                out=ratio[:], in0=var_eps[:, 0:1], scalar1=rstd[:, 0:1], scalar2=rstd[:, 1:2],
+                op0=ALU.mult, op1=ALU.mult,
+            )
+            return rstd, ratio, shift
+
+        def finish(m, v, factors):
+            rstd, ratio, shift = factors
+            gate = stage.tile([P, GATES], F32, name="gate")
+            width = GATES // STORE_CHUNKS
+            for c in range(STORE_CHUNKS):
+                cols = slice(c * width, (c + 1) * width)
+                nc.vector.scalar_tensor_tensor(
+                    out=gate[:, cols], in0=v[:, 1, cols], scalar=ratio[:, 0:1], in1=v[:, 0, cols],
+                    op0=ALU.mult, op1=ALU.add,
+                )
+                nc.scalar.activation(
+                    out=gate[:, cols], in_=gate[:, cols], func=ACT.Sigmoid,
+                    bias=shift[:, 0:1], scale=rstd[:, 0:1],
+                )
+                nc.sync.dma_start(out=out[m * P : (m + 1) * P, cols], in_=gate[:, cols])
+
+        packed = quantise(turn(0))
+        waiting = None
+        for m in range(ROW_TILES):
+            v = stage.tile([P, BRANCHES, GATES], F32, name="v")
+            neg_mean = small.tile([P, BRANCHES], F32, name="neg_mean")
+            sum_sq = small.tile([P, BRANCHES], F32, name="sum_sq")
+            sums0 = small.tile([P, BANKS], F32, name="sums0")
+            sums1 = small.tile([P, BANKS], F32, name="sums1")
+
+            product(0, packed, v, sums0)
+            grouped = turn(m + 1) if m + 1 < ROW_TILES else None
+            spread(0, v, sums0, neg_mean, sum_sq)
+            product(1, packed, v, sums1)
+            spread(1, v, sums1, neg_mean, sum_sq)
+            if grouped is not None:
+                packed = quantise(grouped)
+            factors = row_factors(neg_mean, sum_sq)
+            if waiting is not None:
+                finish(*waiting)
+            waiting = (m, v, factors)
+        finish(*waiting)

@@ -26,6 +26,7 @@ BANK = 512
 BANKS = GATES // BANK
 HALVES = 2
 STORE_CHUNKS = 2
+LAG = 2
 
 FLOPS = 2 * BRANCHES * ROWS * K * GATES
 
@@ -42,7 +43,8 @@ def tile_layernormgrucell_pa_kernel(
     with ExitStack() as ctx:
         keep = ctx.enter_context(tc.tile_pool(name="keep", bufs=1))
         stage = ctx.enter_context(tc.tile_pool(name="stage", bufs=2))
-        small = ctx.enter_context(tc.tile_pool(name="small", bufs=3))
+        rows_pool = ctx.enter_context(tc.tile_pool(name="rows", bufs=LAG + 1))
+        small = ctx.enter_context(tc.tile_pool(name="small", bufs=LAG + 2))
         acc_pool = ctx.enter_context(tc.psum_pool(name="acc", bufs=6))
         turn_pool = ctx.enter_context(tc.psum_pool(name="turn", bufs=2))
         ctx.enter_context(tc.manual_schedule())
@@ -208,9 +210,9 @@ def tile_layernormgrucell_pa_kernel(
                 nc.sync.dma_start(out=out[m * P : (m + 1) * P, cols], in_=gate[:, cols])
 
         packed = quantise(turn(0))
-        waiting = None
+        waiting = {}
         for m in range(ROW_TILES):
-            v = stage.tile([P, BRANCHES, GATES], F32, name="v")
+            v = rows_pool.tile([P, BRANCHES, GATES], F32, name="v")
             neg_mean = small.tile([P, BRANCHES], F32, name="neg_mean")
             sum_sq = small.tile([P, BRANCHES], F32, name="sum_sq")
             sums0 = small.tile([P, BANKS], F32, name="sums0")
@@ -223,8 +225,8 @@ def tile_layernormgrucell_pa_kernel(
             spread(1, v, sums1, neg_mean, sum_sq)
             if grouped is not None:
                 packed = quantise(grouped)
-            factors = row_factors(neg_mean, sum_sq)
-            if waiting is not None:
-                finish(*waiting)
-            waiting = (m, v, factors)
-        finish(*waiting)
+            waiting[m] = (v, row_factors(neg_mean, sum_sq))
+            if m >= LAG:
+                finish(m - LAG, *waiting[m - LAG])
+        for m in range(ROW_TILES - LAG, ROW_TILES):
+            finish(m, *waiting[m])

@@ -26,7 +26,6 @@ BANK = 512
 BANKS = GATES // BANK
 HALVES = 2
 STORE_CHUNKS = 2
-LAG = 2
 
 FLOPS = 2 * BRANCHES * ROWS * K * GATES
 
@@ -43,8 +42,7 @@ def tile_layernormgrucell_pa_kernel(
     with ExitStack() as ctx:
         keep = ctx.enter_context(tc.tile_pool(name="keep", bufs=1))
         stage = ctx.enter_context(tc.tile_pool(name="stage", bufs=2))
-        rows_pool = ctx.enter_context(tc.tile_pool(name="rows", bufs=LAG + 1))
-        small = ctx.enter_context(tc.tile_pool(name="small", bufs=LAG + 2))
+        small = ctx.enter_context(tc.tile_pool(name="small", bufs=3))
         acc_pool = ctx.enter_context(tc.psum_pool(name="acc", bufs=6))
         turn_pool = ctx.enter_context(tc.psum_pool(name="turn", bufs=2))
         ctx.enter_context(tc.manual_schedule())
@@ -52,12 +50,16 @@ def tile_layernormgrucell_pa_kernel(
         raw = keep.tile([P, BRANCHES, ROW_TILES, K], BF16)
         w_words = keep.tile([P, BRANCHES, PASSES, 2 * GATES], U8, align_bytes=64)
         w_planes = keep.tile([P, BRANCHES, PASSES, GATES], U8, align_bytes=64)
+        bias_rows = keep.tile([P, BRANCHES, GATES], BF16)
         bias_all = keep.tile([P, BRANCHES, GATES], BF16)
+        ones = keep.tile([P, P], BF16)
         ident = keep.tile([P, P], F32)
         minus_half = keep.tile([P, BRANCHES], F32)
         warm = keep.tile([P, 1], F32)
 
         nc.vector.memset(w_planes[:].bitcast(I32), 0)
+        nc.vector.memset(bias_rows[:], 0.0)
+        nc.vector.memset(ones[:], 1.0)
         nc.vector.memset(minus_half[:], -0.5)
         make_identity(nc, ident[:])
         nc.scalar.activation(out=warm[:], in_=minus_half[:, 0:1], func=ACT.Sigmoid)
@@ -85,9 +87,10 @@ def tile_layernormgrucell_pa_kernel(
                     out=words[:, b, :, n * step : (n + 1) * step],
                     in_=source[:, :, n * step : (n + 1) * step].rearrange("g p c -> p g c"),
                 )
-            nc.sync.dma_start(out=bias_all[:, b, :], in_=biases[b].partition_broadcast(P))
 
         load_rows(0)
+        for b in range(BRANCHES):
+            nc.scalar.dma_start(out=bias_rows[0:1, b, :], in_=biases[b].unsqueeze(0))
         load_scales(0)
         load_scales(1)
         load_words(0)
@@ -116,6 +119,19 @@ def tile_layernormgrucell_pa_kernel(
                 )
                 grouped.append(side)
             return grouped
+
+        def repeat_biases():
+            for b in range(BRANCHES):
+                for n in range(BANKS):
+                    cols = slice(n * BANK, (n + 1) * BANK)
+                    acc = acc_pool.tile([P, BANK], F32, name="acc")
+                    nc.tensor.matmul(
+                        out=acc[:], lhsT=ones[:], rhs=bias_rows[:, b, cols], start=True, stop=True
+                    )
+                    if n % 2 == 0:
+                        nc.vector.tensor_copy(out=bias_all[:, b, cols], in_=acc[:])
+                    else:
+                        nc.scalar.copy(out=bias_all[:, b, cols], in_=acc[:])
 
         def quantise(grouped):
             packed = []
@@ -210,9 +226,10 @@ def tile_layernormgrucell_pa_kernel(
                 nc.sync.dma_start(out=out[m * P : (m + 1) * P, cols], in_=gate[:, cols])
 
         packed = quantise(turn(0))
-        waiting = {}
+        repeat_biases()
+        waiting = None
         for m in range(ROW_TILES):
-            v = rows_pool.tile([P, BRANCHES, GATES], F32, name="v")
+            v = stage.tile([P, BRANCHES, GATES], F32, name="v")
             neg_mean = small.tile([P, BRANCHES], F32, name="neg_mean")
             sum_sq = small.tile([P, BRANCHES], F32, name="sum_sq")
             sums0 = small.tile([P, BANKS], F32, name="sums0")
@@ -225,8 +242,8 @@ def tile_layernormgrucell_pa_kernel(
             spread(1, v, sums1, neg_mean, sum_sq)
             if grouped is not None:
                 packed = quantise(grouped)
-            waiting[m] = (v, row_factors(neg_mean, sum_sq))
-            if m >= LAG:
-                finish(m - LAG, *waiting[m - LAG])
-        for m in range(ROW_TILES - LAG, ROW_TILES):
-            finish(m, *waiting[m])
+            factors = row_factors(neg_mean, sum_sq)
+            if waiting is not None:
+                finish(*waiting)
+            waiting = (m, v, factors)
+        finish(*waiting)

@@ -57,8 +57,9 @@ def tile_layernormgrucell_pa_kernel(
         minus_half = keep.tile([P, BRANCHES], F32)
         warm = keep.tile([P, 1], F32)
 
-        nc.vector.memset(w_planes[:].bitcast(I32), 0)
-        nc.vector.memset(bias_rows[:], 0.0)
+        for b in range(BRANCHES):
+            nc.vector.memset(bias_rows[:, b, :], 0.0)
+            nc.vector.memset(w_planes[:, b, :, :].bitcast(I32), 0)
         nc.vector.memset(ones[:], 1.0)
         nc.vector.memset(minus_half[:], -0.5)
         make_identity(nc, ident[:])
@@ -71,11 +72,10 @@ def tile_layernormgrucell_pa_kernel(
         def load_scales(b):
             planes = w_planes[:].bitcast(I32)
             rows = weight_scales[b].bitcast(I32)
-            for q in range(8):
-                first = 32 * (q // 4) + q % 4
+            for r in range(4):
                 nc.sync.dma_start(
-                    out=planes[first : P : 64, b, :, :],
-                    in_=rows[:, q : 16 : 8, :].rearrange("g q c -> q g c"),
+                    out=planes[r : P : 32, b, :, :],
+                    in_=rows[:, r : 16 : 4, :].rearrange("g q c -> q g c"),
                 )
 
         def load_words(b):
@@ -92,8 +92,8 @@ def tile_layernormgrucell_pa_kernel(
         for b in range(BRANCHES):
             nc.scalar.dma_start(out=bias_rows[0:1, b, :], in_=biases[b].unsqueeze(0))
         load_scales(0)
-        load_scales(1)
         load_words(0)
+        load_scales(1)
         load_rows(1)
         load_words(1)
         for m in range(2, ROW_TILES):
@@ -120,18 +120,17 @@ def tile_layernormgrucell_pa_kernel(
                 grouped.append(side)
             return grouped
 
-        def repeat_biases():
-            for b in range(BRANCHES):
-                for n in range(BANKS):
-                    cols = slice(n * BANK, (n + 1) * BANK)
-                    acc = acc_pool.tile([P, BANK], F32, name="acc")
-                    nc.tensor.matmul(
-                        out=acc[:], lhsT=ones[:], rhs=bias_rows[:, b, cols], start=True, stop=True
-                    )
-                    if n % 2 == 0:
-                        nc.vector.tensor_copy(out=bias_all[:, b, cols], in_=acc[:])
-                    else:
-                        nc.scalar.copy(out=bias_all[:, b, cols], in_=acc[:])
+        def repeat_bias(b):
+            for n in range(BANKS):
+                cols = slice(n * BANK, (n + 1) * BANK)
+                acc = acc_pool.tile([P, BANK], F32, name="acc")
+                nc.tensor.matmul(
+                    out=acc[:], lhsT=ones[:], rhs=bias_rows[:, b, cols], start=True, stop=True
+                )
+                if n % 2 == 0:
+                    nc.vector.tensor_copy(out=bias_all[:, b, cols], in_=acc[:])
+                else:
+                    nc.scalar.copy(out=bias_all[:, b, cols], in_=acc[:])
 
         def quantise(grouped):
             packed = []
@@ -201,12 +200,12 @@ def tile_layernormgrucell_pa_kernel(
                 op0=ALU.mult, op1=ALU.add,
             )
             nc.gpsimd.tensor_tensor(out=rstd[:], in0=var_eps[:], in1=minus_half[:], op=ALU.pow)
-            nc.gpsimd.tensor_tensor(out=parts[:], in0=rstd[:], in1=neg_mean[:], op=ALU.mult)
-            nc.gpsimd.tensor_tensor(out=shift[:], in0=parts[:, 0:1], in1=parts[:, 1:2], op=ALU.add)
             nc.gpsimd.tensor_scalar(
                 out=ratio[:], in0=var_eps[:, 0:1], scalar1=rstd[:, 0:1], scalar2=rstd[:, 1:2],
                 op0=ALU.mult, op1=ALU.mult,
             )
+            nc.gpsimd.tensor_tensor(out=parts[:], in0=rstd[:], in1=neg_mean[:], op=ALU.mult)
+            nc.gpsimd.tensor_tensor(out=shift[:], in0=parts[:, 0:1], in1=parts[:, 1:2], op=ALU.add)
             return rstd, ratio, shift
 
         def finish(m, v, factors):
@@ -226,7 +225,7 @@ def tile_layernormgrucell_pa_kernel(
                 nc.sync.dma_start(out=out[m * P : (m + 1) * P, cols], in_=gate[:, cols])
 
         packed = quantise(turn(0))
-        repeat_biases()
+        repeat_bias(0)
         waiting = None
         for m in range(ROW_TILES):
             v = stage.tile([P, BRANCHES, GATES], F32, name="v")
@@ -236,6 +235,8 @@ def tile_layernormgrucell_pa_kernel(
             sums1 = small.tile([P, BANKS], F32, name="sums1")
 
             product(0, packed, v, sums0)
+            if m == 0:
+                repeat_bias(1)
             grouped = turn(m + 1) if m + 1 < ROW_TILES else None
             spread(0, v, sums0, neg_mean, sum_sq)
             product(1, packed, v, sums1)

@@ -143,7 +143,7 @@ def tile_layernormgrucell_pa_kernel(
                 packed.append((codes, plane))
             return packed
 
-        def product(b, packed, v, sums):
+        def product(b, packed, v, sums, neg_centre):
             codes, plane = packed[b]
             for n in range(BANKS):
                 acc = acc_pool.tile([P, BANK], F32, name="acc")
@@ -165,48 +165,68 @@ def tile_layernormgrucell_pa_kernel(
                     in1=bias_all[:, b, cols],
                     op0=ALU.mult,
                     op1=ALU.add,
-                    accum_out=sums[:, n : n + 1],
+                    accum_out=sums[:, b, n : n + 1],
                 )
+                if n == 0:
+                    nc.gpsimd.tensor_scalar(
+                        out=neg_centre[:, b : b + 1], in0=sums[:, b, 0:1],
+                        scalar1=-1.0 / BANK, scalar2=0.0, op0=ALU.mult, op1=ALU.add,
+                    )
 
-        def spread(b, v, sums, neg_mean, sum_sq):
-            pair = small.tile([P, 2], F32, name="pair")
-            nc.gpsimd.tensor_tensor(out=pair[:], in0=sums[:, 0:2], in1=sums[:, 2:4], op=ALU.add)
-            nc.gpsimd.tensor_scalar(
-                out=neg_mean[:, b : b + 1],
-                in0=pair[:, 0:1],
-                scalar1=pair[:, 1:2],
-                scalar2=-1.0 / GATES,
-                op0=ALU.add,
-                op1=ALU.mult,
-            )
+        def spread(b, v, neg_centre, sum_sq):
             squares = stage.tile([P, GATES], BF16, name="squares")
             nc.scalar.activation(
                 out=squares[:],
                 in_=v[:, b, :],
                 func=ACT.Square,
-                bias=neg_mean[:, b : b + 1],
+                bias=neg_centre[:, b : b + 1],
                 scale=1.0,
                 accum_out=sum_sq[:, b : b + 1],
             )
 
-        def row_factors(neg_mean, sum_sq):
-            var_eps = small.tile([P, BRANCHES], F32, name="var_eps")
-            rstd = small.tile([P, BRANCHES], F32, name="rstd")
-            parts = small.tile([P, BRANCHES], F32, name="parts")
-            shift = small.tile([P, 1], F32, name="shift")
-            ratio = small.tile([P, 1], F32, name="ratio")
+        def row_means(sums, neg_centre):
+            pairs = small.tile([P, BRANCHES, 2], F32, name="pairs")
+            total = small.tile([P, BRANCHES], F32, name="total")
+            neg_mean = small.tile([P, BRANCHES], F32, name="neg_mean")
+            off = small.tile([P, BRANCHES], F32, name="off")
+            off_sq = small.tile([P, BRANCHES], F32, name="off_sq")
+            nc.gpsimd.tensor_tensor(
+                out=pairs[:], in0=sums[:, :, 0:2], in1=sums[:, :, 2:4], op=ALU.add
+            )
+            nc.gpsimd.tensor_tensor(
+                out=total[:], in0=pairs[:, :, 0], in1=pairs[:, :, 1], op=ALU.add
+            )
             nc.gpsimd.tensor_scalar(
-                out=var_eps[:], in0=sum_sq[:], scalar1=1.0 / GATES, scalar2=EPS,
+                out=neg_mean[:], in0=total[:], scalar1=-1.0 / GATES, scalar2=0.0,
                 op0=ALU.mult, op1=ALU.add,
             )
+            nc.gpsimd.tensor_tensor(out=off[:], in0=neg_mean[:], in1=neg_centre[:], op=ALU.subtract)
+            nc.gpsimd.tensor_tensor(out=off_sq[:], in0=off[:], in1=off[:], op=ALU.mult)
+            return neg_mean, off_sq
+
+        def row_scales(off_sq, sum_sq):
+            raw_eps = small.tile([P, BRANCHES], F32, name="raw_eps")
+            var_eps = small.tile([P, BRANCHES], F32, name="var_eps")
+            rstd = small.tile([P, BRANCHES], F32, name="rstd")
+            ratio = small.tile([P, 1], F32, name="ratio")
+            nc.gpsimd.tensor_scalar(
+                out=raw_eps[:], in0=sum_sq[:], scalar1=1.0 / GATES, scalar2=EPS,
+                op0=ALU.mult, op1=ALU.add,
+            )
+            nc.gpsimd.tensor_tensor(out=var_eps[:], in0=raw_eps[:], in1=off_sq[:], op=ALU.subtract)
             nc.gpsimd.tensor_tensor(out=rstd[:], in0=var_eps[:], in1=minus_half[:], op=ALU.pow)
             nc.gpsimd.tensor_scalar(
                 out=ratio[:], in0=var_eps[:, 0:1], scalar1=rstd[:, 0:1], scalar2=rstd[:, 1:2],
                 op0=ALU.mult, op1=ALU.mult,
             )
+            return rstd, ratio
+
+        def row_shift(rstd, neg_mean):
+            parts = small.tile([P, BRANCHES], F32, name="parts")
+            shift = small.tile([P, 1], F32, name="shift")
             nc.gpsimd.tensor_tensor(out=parts[:], in0=rstd[:], in1=neg_mean[:], op=ALU.mult)
             nc.gpsimd.tensor_tensor(out=shift[:], in0=parts[:, 0:1], in1=parts[:, 1:2], op=ALU.add)
-            return rstd, ratio, shift
+            return shift
 
         def finish(m, v, factors):
             rstd, ratio, shift = factors
@@ -226,25 +246,30 @@ def tile_layernormgrucell_pa_kernel(
 
         packed = quantise(turn(0))
         repeat_bias(0)
-        waiting = None
-        for m in range(ROW_TILES):
-            v = stage.tile([P, BRANCHES, GATES], F32, name="v")
-            neg_mean = small.tile([P, BRANCHES], F32, name="neg_mean")
-            sum_sq = small.tile([P, BRANCHES], F32, name="sum_sq")
-            sums0 = small.tile([P, BANKS], F32, name="sums0")
-            sums1 = small.tile([P, BANKS], F32, name="sums1")
-
-            product(0, packed, v, sums0)
+        before = None
+        for m in range(ROW_TILES + 1):
+            if m < ROW_TILES:
+                v = stage.tile([P, BRANCHES, GATES], F32, name="v")
+                neg_centre = small.tile([P, BRANCHES], F32, name="neg_centre")
+                sum_sq = small.tile([P, BRANCHES], F32, name="sum_sq")
+                sums = small.tile([P, BRANCHES, BANKS], F32, name="sums")
+                product(0, packed, v, sums, neg_centre)
             if m == 0:
                 repeat_bias(1)
-            grouped = turn(m + 1) if m + 1 < ROW_TILES else None
-            spread(0, v, sums0, neg_mean, sum_sq)
-            product(1, packed, v, sums1)
-            spread(1, v, sums1, neg_mean, sum_sq)
-            if grouped is not None:
-                packed = quantise(grouped)
-            factors = row_factors(neg_mean, sum_sq)
-            if waiting is not None:
-                finish(*waiting)
-            waiting = (m, v, factors)
-        finish(*waiting)
+            if before is not None:
+                neg_mean, off_sq = row_means(before["sums"], before["neg_centre"])
+                rstd, ratio = row_scales(off_sq, before["sum_sq"])
+            if m < ROW_TILES:
+                grouped = turn(m + 1) if m + 1 < ROW_TILES else None
+                spread(0, v, neg_centre, sum_sq)
+                product(1, packed, v, sums, neg_centre)
+            if before is not None:
+                shift = row_shift(rstd, neg_mean)
+            if m < ROW_TILES:
+                spread(1, v, neg_centre, sum_sq)
+                if grouped is not None:
+                    packed = quantise(grouped)
+            if before is not None:
+                finish(m - 1, before["v"], (rstd, ratio, shift))
+            if m < ROW_TILES:
+                before = {"v": v, "sums": sums, "neg_centre": neg_centre, "sum_sq": sum_sq}

@@ -26,6 +26,11 @@ BANK = 512
 BANKS = GATES // BANK
 HALVES = 2
 STORE_CHUNKS = 2
+WARM_UP = 4
+LAST_CHUNKS = 4
+SPAN = 1
+SPANS = BANKS // SPAN
+ACC_SPANS = 6 // SPAN
 
 FLOPS = 2 * BRANCHES * ROWS * K * GATES
 
@@ -42,8 +47,9 @@ def tile_layernormgrucell_pa_kernel(
     with ExitStack() as ctx:
         keep = ctx.enter_context(tc.tile_pool(name="keep", bufs=1))
         stage = ctx.enter_context(tc.tile_pool(name="stage", bufs=2))
-        small = ctx.enter_context(tc.tile_pool(name="small", bufs=3))
-        acc_pool = ctx.enter_context(tc.psum_pool(name="acc", bufs=6))
+        rows3 = ctx.enter_context(tc.tile_pool(name="rows3", bufs=3))
+        small = ctx.enter_context(tc.tile_pool(name="small", bufs=4))
+        acc_pool = ctx.enter_context(tc.psum_pool(name="acc", bufs=ACC_SPANS))
         turn_pool = ctx.enter_context(tc.psum_pool(name="turn", bufs=2))
         ctx.enter_context(tc.manual_schedule())
 
@@ -52,16 +58,16 @@ def tile_layernormgrucell_pa_kernel(
         w_planes = keep.tile([P, BRANCHES, PASSES, GATES], U8, align_bytes=64)
         bias_rows = keep.tile([P, BRANCHES, GATES], BF16)
         bias_all = keep.tile([P, BRANCHES, GATES], BF16)
-        ones = keep.tile([P, P], BF16)
+        ones = keep.tile([P, BANK], BF16)
         ident = keep.tile([P, P], F32)
         minus_half = keep.tile([P, BRANCHES], F32)
         warm = keep.tile([P, 1], F32)
 
-        for b in range(BRANCHES):
-            nc.vector.memset(bias_rows[:, b, :], 0.0)
-            nc.vector.memset(w_planes[:, b, :, :].bitcast(I32), 0)
-        nc.vector.memset(ones[:], 1.0)
         nc.vector.memset(minus_half[:], -0.5)
+        nc.vector.memset(ones[:], 1.0)
+        for b in range(BRANCHES):
+            nc.vector.memset(w_planes[:, b, :, :].bitcast(I32), 0)
+            nc.vector.memset(bias_rows[:, b, :], 0.0)
         make_identity(nc, ident[:])
         nc.scalar.activation(out=warm[:], in_=minus_half[:, 0:1], func=ACT.Sigmoid)
 
@@ -99,8 +105,15 @@ def tile_layernormgrucell_pa_kernel(
         for m in range(2, ROW_TILES):
             load_rows(m)
 
-        def turn(m):
-            grouped = []
+        turned_of = {}
+        sides_of = {}
+        packed_of = {}
+        rows_of = {}
+        spans = {}
+        progress = {"next": 0, "open": 0}
+
+        def transposes(m):
+            both = []
             for b in range(BRANCHES):
                 words = raw[:, b, m, :].bitcast(F32)
                 turned = turn_pool.tile([P, PASSES * HALVES, P], F32, name="turned")
@@ -112,87 +125,150 @@ def tile_layernormgrucell_pa_kernel(
                             words[:, first : (g + 1) * K_PASS // 2 : HALVES],
                             ident[:],
                         )
+                both.append(turned)
+            turned_of[m] = both
+
+        def copy_turned(m):
+            sides = []
+            for b in range(BRANCHES):
                 side = stage.tile([P, PASSES * P * 4], BF16, align_bytes=64, name="side%d" % b)
                 nc.scalar.copy(
                     out=side[:].bitcast(F32).rearrange("p (g r u) -> p g r u", g=PASSES, u=HALVES),
-                    in_=turned[:].rearrange("p (g u) r -> p g r u", u=HALVES),
+                    in_=turned_of[m][b][:].rearrange("p (g u) r -> p g r u", u=HALVES),
                 )
-                grouped.append(side)
-            return grouped
+                sides.append(side)
+            sides_of[m] = sides
 
-        def repeat_bias(b):
-            for n in range(BANKS):
-                cols = slice(n * BANK, (n + 1) * BANK)
-                acc = acc_pool.tile([P, BANK], F32, name="acc")
-                nc.tensor.matmul(
-                    out=acc[:], lhsT=ones[:], rhs=bias_rows[:, b, cols], start=True, stop=True
-                )
-                if n % 2 == 0:
-                    nc.vector.tensor_copy(out=bias_all[:, b, cols], in_=acc[:])
-                else:
-                    nc.scalar.copy(out=bias_all[:, b, cols], in_=acc[:])
-
-        def quantise(grouped):
+        def quantise(m):
             packed = []
             for b in range(BRANCHES):
-                codes = stage.tile([P, PASSES * P], U32, align_bytes=64, name="codes%d" % b)
-                plane = stage.tile([P, PASSES * P], U8, align_bytes=64, name="plane%d" % b)
+                codes = rows3.tile([P, PASSES * P], U32, align_bytes=64, name="codes%d" % b)
+                plane = rows3.tile([P, PASSES * P], U8, align_bytes=64, name="plane%d" % b)
                 nc.vector.quantize_mx(
-                    out=codes[:].bitcast(FP8X4), scales=plane[:], in_=grouped[b][:]
+                    out=codes[:].bitcast(FP8X4), scales=plane[:], in_=sides_of[m][b][:]
                 )
                 packed.append((codes, plane))
-            return packed
+            packed_of[m] = packed
 
-        def product(b, packed, v, sums, neg_centre):
-            codes, plane = packed[b]
-            for n in range(BANKS):
-                acc = acc_pool.tile([P, BANK], F32, name="acc")
-                for g in range(PASSES):
-                    nc.tensor.matmul_mx(
-                        out=acc[:],
-                        lhsT=codes[:, g * P : (g + 1) * P].bitcast(FP8X4),
-                        lhsT_scale=plane[:, g * P : (g + 1) * P],
-                        rhs=w_words[:, b, g, n * 2 * BANK : (n + 1) * 2 * BANK].bitcast(FP4X4),
-                        rhs_scale=w_planes[:, b, g, n * BANK : (n + 1) * BANK],
-                        start=(g == 0),
-                        stop=(g == PASSES - 1),
+        def tensor_job(job):
+            kind = job[0]
+            if kind == "turn":
+                transposes(job[1])
+                return
+            acc = acc_pool.tile([P, SPAN * BANK], F32, name="acc")
+            spans[job] = acc
+            progress["open"] += 1
+            for i in range(SPAN):
+                part = acc[:, i * BANK : (i + 1) * BANK]
+                if kind == "bias":
+                    b, n = job[1], job[2] * SPAN + i
+                    nc.tensor.matmul(
+                        out=part, lhsT=ones[:, 0:P], rhs=bias_rows[:, b, n * BANK : (n + 1) * BANK],
+                        start=True, stop=True,
                     )
+                else:
+                    m, b, n = job[1], job[2], job[3] * SPAN + i
+                    codes, plane = packed_of[m][b]
+                    for g in range(PASSES):
+                        nc.tensor.matmul_mx(
+                            out=part,
+                            lhsT=codes[:, g * P : (g + 1) * P].bitcast(FP8X4),
+                            lhsT_scale=plane[:, g * P : (g + 1) * P],
+                            rhs=w_words[:, b, g, n * 2 * BANK : (n + 1) * 2 * BANK].bitcast(FP4X4),
+                            rhs_scale=w_planes[:, b, g, n * BANK : (n + 1) * BANK],
+                            start=(g == 0),
+                            stop=(g == PASSES - 1),
+                        )
+
+        jobs = []
+        jobs.extend([("bias", 0, s) for s in range(SPANS)])
+        jobs.extend([("mm", 0, 0, s) for s in range(SPANS)])
+        jobs.append(("turn", 1))
+        jobs.extend([("bias", 1, s) for s in range(SPANS)])
+        jobs.extend([("mm", 0, 1, s) for s in range(SPANS)])
+        jobs.append(("turn", 2))
+        for m in range(1, ROW_TILES):
+            for b in range(BRANCHES):
+                jobs.extend([("mm", m, b, s) for s in range(SPANS)])
+            if m + 2 < ROW_TILES:
+                jobs.append(("turn", m + 2))
+
+        def fill():
+            while progress["next"] < len(jobs):
+                job = jobs[progress["next"]]
+                if job[0] != "turn" and progress["open"] >= ACC_SPANS:
+                    break
+                tensor_job(job)
+                progress["next"] += 1
+
+        def copy_bias(b, s, on_vector):
+            acc = spans[("bias", b, s)]
+            for i in range(SPAN):
+                n = s * SPAN + i
                 cols = slice(n * BANK, (n + 1) * BANK)
+                part = acc[:, i * BANK : (i + 1) * BANK]
+                if on_vector:
+                    nc.vector.tensor_copy(out=bias_all[:, b, cols], in_=part)
+                else:
+                    nc.scalar.copy(out=bias_all[:, b, cols], in_=part)
+            progress["open"] -= 1
+            fill()
+
+        def start_rows(m):
+            rows_of[m] = {
+                "v": rows3.tile([P, BRANCHES, GATES], F32, name="v"),
+                "neg_centre": small.tile([P, BRANCHES], F32, name="neg_centre"),
+                "sum_sq": small.tile([P, BRANCHES], F32, name="sum_sq"),
+                "sums": small.tile([P, BRANCHES, SPANS], F32, name="sums"),
+            }
+
+        def evacuate(m, b):
+            row = rows_of[m]
+            for s in range(SPANS):
+                cols = slice(s * SPAN * BANK, (s + 1) * SPAN * BANK)
                 nc.vector.scalar_tensor_tensor(
-                    out=v[:, b, cols],
-                    in0=acc[:],
+                    out=row["v"][:, b, cols],
+                    in0=spans[("mm", m, b, s)][:],
                     scalar=1.0,
                     in1=bias_all[:, b, cols],
                     op0=ALU.mult,
                     op1=ALU.add,
-                    accum_out=sums[:, b, n : n + 1],
+                    accum_out=row["sums"][:, b, s : s + 1],
                 )
-                if n == 0:
+                progress["open"] -= 1
+                fill()
+                if s == 0:
                     nc.gpsimd.tensor_scalar(
-                        out=neg_centre[:, b : b + 1], in0=sums[:, b, 0:1],
-                        scalar1=-1.0 / BANK, scalar2=0.0, op0=ALU.mult, op1=ALU.add,
+                        out=row["neg_centre"][:, b : b + 1], in0=row["sums"][:, b, 0:1],
+                        scalar1=-1.0 / (SPAN * BANK), scalar2=0.0, op0=ALU.mult, op1=ALU.add,
                     )
 
-        def spread(b, v, neg_centre, sum_sq):
+        def square(m, b):
+            row = rows_of[m]
             squares = stage.tile([P, GATES], BF16, name="squares")
             nc.scalar.activation(
                 out=squares[:],
-                in_=v[:, b, :],
+                in_=row["v"][:, b, :],
                 func=ACT.Square,
-                bias=neg_centre[:, b : b + 1],
+                bias=row["neg_centre"][:, b : b + 1],
                 scale=1.0,
-                accum_out=sum_sq[:, b : b + 1],
+                accum_out=row["sum_sq"][:, b : b + 1],
             )
 
-        def row_means(sums, neg_centre):
-            pairs = small.tile([P, BRANCHES, 2], F32, name="pairs")
+        def row_means(m):
+            row = rows_of[m]
+            sums = row["sums"]
             total = small.tile([P, BRANCHES], F32, name="total")
             neg_mean = small.tile([P, BRANCHES], F32, name="neg_mean")
             off = small.tile([P, BRANCHES], F32, name="off")
             off_sq = small.tile([P, BRANCHES], F32, name="off_sq")
-            nc.gpsimd.tensor_tensor(
-                out=pairs[:], in0=sums[:, :, 0:2], in1=sums[:, :, 2:4], op=ALU.add
-            )
+            if SPANS == 4:
+                pairs = small.tile([P, BRANCHES, 2], F32, name="pairs")
+                nc.gpsimd.tensor_tensor(
+                    out=pairs[:], in0=sums[:, :, 0:2], in1=sums[:, :, 2:4], op=ALU.add
+                )
+            else:
+                pairs = sums
             nc.gpsimd.tensor_tensor(
                 out=total[:], in0=pairs[:, :, 0], in1=pairs[:, :, 1], op=ALU.add
             )
@@ -200,76 +276,92 @@ def tile_layernormgrucell_pa_kernel(
                 out=neg_mean[:], in0=total[:], scalar1=-1.0 / GATES, scalar2=0.0,
                 op0=ALU.mult, op1=ALU.add,
             )
-            nc.gpsimd.tensor_tensor(out=off[:], in0=neg_mean[:], in1=neg_centre[:], op=ALU.subtract)
+            nc.gpsimd.tensor_tensor(
+                out=off[:], in0=neg_mean[:], in1=row["neg_centre"][:], op=ALU.subtract
+            )
             nc.gpsimd.tensor_tensor(out=off_sq[:], in0=off[:], in1=off[:], op=ALU.mult)
-            return neg_mean, off_sq
+            row["neg_mean"] = neg_mean
+            row["off_sq"] = off_sq
 
-        def row_scales(off_sq, sum_sq):
+        def row_scales(m):
+            row = rows_of[m]
             raw_eps = small.tile([P, BRANCHES], F32, name="raw_eps")
             var_eps = small.tile([P, BRANCHES], F32, name="var_eps")
             rstd = small.tile([P, BRANCHES], F32, name="rstd")
             ratio = small.tile([P, 1], F32, name="ratio")
             nc.gpsimd.tensor_scalar(
-                out=raw_eps[:], in0=sum_sq[:], scalar1=1.0 / GATES, scalar2=EPS,
+                out=raw_eps[:], in0=row["sum_sq"][:], scalar1=1.0 / GATES, scalar2=EPS,
                 op0=ALU.mult, op1=ALU.add,
             )
-            nc.gpsimd.tensor_tensor(out=var_eps[:], in0=raw_eps[:], in1=off_sq[:], op=ALU.subtract)
+            nc.gpsimd.tensor_tensor(
+                out=var_eps[:], in0=raw_eps[:], in1=row["off_sq"][:], op=ALU.subtract
+            )
             nc.gpsimd.tensor_tensor(out=rstd[:], in0=var_eps[:], in1=minus_half[:], op=ALU.pow)
             nc.gpsimd.tensor_scalar(
                 out=ratio[:], in0=var_eps[:, 0:1], scalar1=rstd[:, 0:1], scalar2=rstd[:, 1:2],
                 op0=ALU.mult, op1=ALU.mult,
             )
-            return rstd, ratio
+            row["rstd"] = rstd
+            row["ratio"] = ratio
 
-        def row_shift(rstd, neg_mean):
+        def row_shift(m):
+            row = rows_of[m]
             parts = small.tile([P, BRANCHES], F32, name="parts")
             shift = small.tile([P, 1], F32, name="shift")
-            nc.gpsimd.tensor_tensor(out=parts[:], in0=rstd[:], in1=neg_mean[:], op=ALU.mult)
+            nc.gpsimd.tensor_tensor(
+                out=parts[:], in0=row["rstd"][:], in1=row["neg_mean"][:], op=ALU.mult
+            )
             nc.gpsimd.tensor_tensor(out=shift[:], in0=parts[:, 0:1], in1=parts[:, 1:2], op=ALU.add)
-            return shift
+            row["shift"] = shift
 
-        def finish(m, v, factors):
-            rstd, ratio, shift = factors
-            gate = stage.tile([P, GATES], F32, name="gate")
-            width = GATES // STORE_CHUNKS
-            for c in range(STORE_CHUNKS):
+        def finish(m, chunks):
+            row = rows_of[m]
+            gate = rows3.tile([P, GATES], F32, name="gate")
+            v = row["v"]
+            width = GATES // chunks
+            for c in range(chunks):
                 cols = slice(c * width, (c + 1) * width)
                 nc.vector.scalar_tensor_tensor(
-                    out=gate[:, cols], in0=v[:, 1, cols], scalar=ratio[:, 0:1], in1=v[:, 0, cols],
-                    op0=ALU.mult, op1=ALU.add,
+                    out=gate[:, cols], in0=v[:, 1, cols], scalar=row["ratio"][:, 0:1],
+                    in1=v[:, 0, cols], op0=ALU.mult, op1=ALU.add,
                 )
                 nc.scalar.activation(
                     out=gate[:, cols], in_=gate[:, cols], func=ACT.Sigmoid,
-                    bias=shift[:, 0:1], scale=rstd[:, 0:1],
+                    bias=row["shift"][:, 0:1], scale=row["rstd"][:, 0:1],
                 )
                 nc.sync.dma_start(out=out[m * P : (m + 1) * P, cols], in_=gate[:, cols])
 
-        packed = quantise(turn(0))
-        repeat_bias(0)
-        before = None
+        idle = turn_pool.tile([P, BANK], F32, name="turned")
+        for i in range(WARM_UP):
+            nc.tensor.matmul(out=idle[:], lhsT=ones[:, 0:P], rhs=ones[:], start=True, stop=True)
+        transposes(0)
+        copy_turned(0)
+        quantise(0)
+        fill()
+        for s in range(SPANS):
+            copy_bias(0, s, s % 2 == 0)
         for m in range(ROW_TILES + 1):
             if m < ROW_TILES:
-                v = stage.tile([P, BRANCHES, GATES], F32, name="v")
-                neg_centre = small.tile([P, BRANCHES], F32, name="neg_centre")
-                sum_sq = small.tile([P, BRANCHES], F32, name="sum_sq")
-                sums = small.tile([P, BRANCHES, BANKS], F32, name="sums")
-                product(0, packed, v, sums, neg_centre)
+                start_rows(m)
+                evacuate(m, 0)
             if m == 0:
-                repeat_bias(1)
-            if before is not None:
-                neg_mean, off_sq = row_means(before["sums"], before["neg_centre"])
-                rstd, ratio = row_scales(off_sq, before["sum_sq"])
+                copy_turned(1)
+                quantise(1)
+                for s in range(SPANS):
+                    copy_bias(1, s, False)
+            if m > 0:
+                row_means(m - 1)
+                row_scales(m - 1)
             if m < ROW_TILES:
-                grouped = turn(m + 1) if m + 1 < ROW_TILES else None
-                spread(0, v, neg_centre, sum_sq)
-                product(1, packed, v, sums, neg_centre)
-            if before is not None:
-                shift = row_shift(rstd, neg_mean)
+                if m + 2 < ROW_TILES:
+                    copy_turned(m + 2)
+                square(m, 0)
+                evacuate(m, 1)
+            if m > 0:
+                row_shift(m - 1)
             if m < ROW_TILES:
-                spread(1, v, neg_centre, sum_sq)
-                if grouped is not None:
-                    packed = quantise(grouped)
-            if before is not None:
-                finish(m - 1, before["v"], (rstd, ratio, shift))
-            if m < ROW_TILES:
-                before = {"v": v, "sums": sums, "neg_centre": neg_centre, "sum_sq": sum_sq}
+                square(m, 1)
+                if m + 2 < ROW_TILES:
+                    quantise(m + 2)
+            if m > 0:
+                finish(m - 1, STORE_CHUNKS if m < ROW_TILES else LAST_CHUNKS)

@@ -26,6 +26,8 @@ BANK = 512
 BANKS = GATES // BANK
 HALVES = 2
 STORE_CHUNKS = 2
+FIRST = 512
+LAG = 2
 WARM_UP = 4
 LAST_CHUNKS = 4
 SPAN = 1
@@ -217,7 +219,6 @@ def tile_layernormgrucell_pa_kernel(
         def start_rows(m):
             rows_of[m] = {
                 "v": rows3.tile([P, BRANCHES, GATES], F32, name="v"),
-                "neg_centre": small.tile([P, BRANCHES], F32, name="neg_centre"),
                 "sum_sq": small.tile([P, BRANCHES], F32, name="sum_sq"),
                 "sums": small.tile([P, BRANCHES, SPANS], F32, name="sums"),
             }
@@ -237,11 +238,6 @@ def tile_layernormgrucell_pa_kernel(
                 )
                 progress["open"] -= 1
                 fill()
-                if s == 0:
-                    nc.gpsimd.tensor_scalar(
-                        out=row["neg_centre"][:, b : b + 1], in0=row["sums"][:, b, 0:1],
-                        scalar1=-1.0 / (SPAN * BANK), scalar2=0.0, op0=ALU.mult, op1=ALU.add,
-                    )
 
         def square(m, b):
             row = rows_of[m]
@@ -250,25 +246,38 @@ def tile_layernormgrucell_pa_kernel(
                 out=squares[:],
                 in_=row["v"][:, b, :],
                 func=ACT.Square,
-                bias=row["neg_centre"][:, b : b + 1],
-                scale=1.0,
+                bias=row["sums"][:, b, 0:1],
+                scale=-float(FIRST),
                 accum_out=row["sum_sq"][:, b : b + 1],
             )
 
-        def row_means(m):
+        def row_stats(m, squares_first):
             row = rows_of[m]
             sums = row["sums"]
+            raw_eps = small.tile([P, BRANCHES], F32, name="raw_eps")
+            pairs = small.tile([P, BRANCHES, 2], F32, name="pairs")
             total = small.tile([P, BRANCHES], F32, name="total")
             neg_mean = small.tile([P, BRANCHES], F32, name="neg_mean")
+            neg_centre = small.tile([P, BRANCHES], F32, name="neg_centre")
             off = small.tile([P, BRANCHES], F32, name="off")
             off_sq = small.tile([P, BRANCHES], F32, name="off_sq")
-            if SPANS == 4:
-                pairs = small.tile([P, BRANCHES, 2], F32, name="pairs")
-                nc.gpsimd.tensor_tensor(
-                    out=pairs[:], in0=sums[:, :, 0:2], in1=sums[:, :, 2:4], op=ALU.add
+            var_eps = small.tile([P, BRANCHES], F32, name="var_eps")
+            rstd = small.tile([P, BRANCHES], F32, name="rstd")
+            ratio = small.tile([P, 1], F32, name="ratio")
+            parts = small.tile([P, BRANCHES], F32, name="parts")
+            shift = small.tile([P, 1], F32, name="shift")
+
+            def from_squares():
+                nc.gpsimd.tensor_scalar(
+                    out=raw_eps[:], in0=row["sum_sq"][:], scalar1=1.0 / (GATES * FIRST * FIRST),
+                    scalar2=EPS, op0=ALU.mult, op1=ALU.add,
                 )
-            else:
-                pairs = sums
+
+            if squares_first:
+                from_squares()
+            nc.gpsimd.tensor_tensor(
+                out=pairs[:], in0=sums[:, :, 0:2], in1=sums[:, :, 2:4], op=ALU.add
+            )
             nc.gpsimd.tensor_tensor(
                 out=total[:], in0=pairs[:, :, 0], in1=pairs[:, :, 1], op=ALU.add
             )
@@ -276,42 +285,24 @@ def tile_layernormgrucell_pa_kernel(
                 out=neg_mean[:], in0=total[:], scalar1=-1.0 / GATES, scalar2=0.0,
                 op0=ALU.mult, op1=ALU.add,
             )
-            nc.gpsimd.tensor_tensor(
-                out=off[:], in0=neg_mean[:], in1=row["neg_centre"][:], op=ALU.subtract
-            )
-            nc.gpsimd.tensor_tensor(out=off_sq[:], in0=off[:], in1=off[:], op=ALU.mult)
-            row["neg_mean"] = neg_mean
-            row["off_sq"] = off_sq
-
-        def row_scales(m):
-            row = rows_of[m]
-            raw_eps = small.tile([P, BRANCHES], F32, name="raw_eps")
-            var_eps = small.tile([P, BRANCHES], F32, name="var_eps")
-            rstd = small.tile([P, BRANCHES], F32, name="rstd")
-            ratio = small.tile([P, 1], F32, name="ratio")
             nc.gpsimd.tensor_scalar(
-                out=raw_eps[:], in0=row["sum_sq"][:], scalar1=1.0 / GATES, scalar2=EPS,
+                out=neg_centre[:], in0=sums[:, :, 0], scalar1=-1.0 / FIRST, scalar2=0.0,
                 op0=ALU.mult, op1=ALU.add,
             )
-            nc.gpsimd.tensor_tensor(
-                out=var_eps[:], in0=raw_eps[:], in1=row["off_sq"][:], op=ALU.subtract
-            )
+            nc.gpsimd.tensor_tensor(out=off[:], in0=neg_mean[:], in1=neg_centre[:], op=ALU.subtract)
+            nc.gpsimd.tensor_tensor(out=off_sq[:], in0=off[:], in1=off[:], op=ALU.mult)
+            if not squares_first:
+                from_squares()
+            nc.gpsimd.tensor_tensor(out=var_eps[:], in0=raw_eps[:], in1=off_sq[:], op=ALU.subtract)
             nc.gpsimd.tensor_tensor(out=rstd[:], in0=var_eps[:], in1=minus_half[:], op=ALU.pow)
             nc.gpsimd.tensor_scalar(
                 out=ratio[:], in0=var_eps[:, 0:1], scalar1=rstd[:, 0:1], scalar2=rstd[:, 1:2],
                 op0=ALU.mult, op1=ALU.mult,
             )
+            nc.gpsimd.tensor_tensor(out=parts[:], in0=rstd[:], in1=neg_mean[:], op=ALU.mult)
+            nc.gpsimd.tensor_tensor(out=shift[:], in0=parts[:, 0:1], in1=parts[:, 1:2], op=ALU.add)
             row["rstd"] = rstd
             row["ratio"] = ratio
-
-        def row_shift(m):
-            row = rows_of[m]
-            parts = small.tile([P, BRANCHES], F32, name="parts")
-            shift = small.tile([P, 1], F32, name="shift")
-            nc.gpsimd.tensor_tensor(
-                out=parts[:], in0=row["rstd"][:], in1=row["neg_mean"][:], op=ALU.mult
-            )
-            nc.gpsimd.tensor_tensor(out=shift[:], in0=parts[:, 0:1], in1=parts[:, 1:2], op=ALU.add)
             row["shift"] = shift
 
         def finish(m, chunks):
@@ -340,7 +331,9 @@ def tile_layernormgrucell_pa_kernel(
         fill()
         for s in range(SPANS):
             copy_bias(0, s, s % 2 == 0)
-        for m in range(ROW_TILES + 1):
+        for m in range(ROW_TILES + LAG):
+            if 0 < m <= ROW_TILES:
+                row_stats(m - 1, m < ROW_TILES)
             if m < ROW_TILES:
                 start_rows(m)
                 evacuate(m, 0)
@@ -349,19 +342,13 @@ def tile_layernormgrucell_pa_kernel(
                 quantise(1)
                 for s in range(SPANS):
                     copy_bias(1, s, False)
-            if m > 0:
-                row_means(m - 1)
-                row_scales(m - 1)
             if m < ROW_TILES:
                 if m + 2 < ROW_TILES:
                     copy_turned(m + 2)
                 square(m, 0)
                 evacuate(m, 1)
-            if m > 0:
-                row_shift(m - 1)
-            if m < ROW_TILES:
                 square(m, 1)
                 if m + 2 < ROW_TILES:
                     quantise(m + 2)
-            if m > 0:
-                finish(m - 1, STORE_CHUNKS if m < ROW_TILES else LAST_CHUNKS)
+            if m >= LAG:
+                finish(m - LAG, STORE_CHUNKS if m - LAG < ROW_TILES - 1 else LAST_CHUNKS)

@@ -28,8 +28,7 @@ HALVES = 2
 STORE_CHUNKS = 2
 FIRST = 512
 LAG = 2
-WARM_UP = 4
-LAST_CHUNKS = 4
+LAST_CHUNKS = 2
 SPAN = 1
 SPANS = BANKS // SPAN
 ACC_SPANS = 6 // SPAN
@@ -60,16 +59,16 @@ def tile_layernormgrucell_pa_kernel(
         w_planes = keep.tile([P, BRANCHES, PASSES, GATES], U8, align_bytes=64)
         bias_rows = keep.tile([P, BRANCHES, GATES], BF16)
         bias_all = keep.tile([P, BRANCHES, GATES], BF16)
-        ones = keep.tile([P, BANK], BF16)
+        ones = keep.tile([P, P], BF16)
         ident = keep.tile([P, P], F32)
         minus_half = keep.tile([P, BRANCHES], F32)
         warm = keep.tile([P, 1], F32)
 
-        nc.vector.memset(minus_half[:], -0.5)
-        nc.vector.memset(ones[:], 1.0)
         for b in range(BRANCHES):
-            nc.vector.memset(w_planes[:, b, :, :].bitcast(I32), 0)
             nc.vector.memset(bias_rows[:, b, :], 0.0)
+            nc.vector.memset(w_planes[:, b, :, :].bitcast(I32), 0)
+        nc.vector.memset(ones[:], 1.0)
+        nc.vector.memset(minus_half[:], -0.5)
         make_identity(nc, ident[:])
         nc.scalar.activation(out=warm[:], in_=minus_half[:, 0:1], func=ACT.Sigmoid)
 
@@ -165,7 +164,7 @@ def tile_layernormgrucell_pa_kernel(
                 if kind == "bias":
                     b, n = job[1], job[2] * SPAN + i
                     nc.tensor.matmul(
-                        out=part, lhsT=ones[:, 0:P], rhs=bias_rows[:, b, n * BANK : (n + 1) * BANK],
+                        out=part, lhsT=ones[:], rhs=bias_rows[:, b, n * BANK : (n + 1) * BANK],
                         start=True, stop=True,
                     )
                 else:
@@ -185,8 +184,8 @@ def tile_layernormgrucell_pa_kernel(
         jobs = []
         jobs.extend([("bias", 0, s) for s in range(SPANS)])
         jobs.extend([("mm", 0, 0, s) for s in range(SPANS)])
-        jobs.append(("turn", 1))
         jobs.extend([("bias", 1, s) for s in range(SPANS)])
+        jobs.append(("turn", 1))
         jobs.extend([("mm", 0, 1, s) for s in range(SPANS)])
         jobs.append(("turn", 2))
         for m in range(1, ROW_TILES):
@@ -322,9 +321,6 @@ def tile_layernormgrucell_pa_kernel(
                 )
                 nc.sync.dma_start(out=out[m * P : (m + 1) * P, cols], in_=gate[:, cols])
 
-        idle = turn_pool.tile([P, BANK], F32, name="turned")
-        for i in range(WARM_UP):
-            nc.tensor.matmul(out=idle[:], lhsT=ones[:, 0:P], rhs=ones[:], start=True, stop=True)
         transposes(0)
         copy_turned(0)
         quantise(0)
@@ -341,7 +337,7 @@ def tile_layernormgrucell_pa_kernel(
                 copy_turned(1)
                 quantise(1)
                 for s in range(SPANS):
-                    copy_bias(1, s, False)
+                    copy_bias(1, s, s % 2 == 0)
             if m < ROW_TILES:
                 if m + 2 < ROW_TILES:
                     copy_turned(m + 2)

@@ -26,6 +26,7 @@ BANK = 512
 BANKS = GATES // BANK
 HALVES = 2
 STORE_CHUNKS = 2
+HALF = 1024
 FIRST = 512
 LAG = 2
 LAST_CHUNKS = 2
@@ -156,35 +157,39 @@ def tile_layernormgrucell_pa_kernel(
             if kind == "turn":
                 transposes(job[1])
                 return
+            progress["open"] += 1
+            if kind == "bias":
+                b, half = job[1], job[2]
+                pair = acc_pool.tile([P, HALF], BF16, name="acc")
+                spans[job] = pair
+                for i in range(HALF // BANK):
+                    cols = slice(half * HALF + i * BANK, half * HALF + (i + 1) * BANK)
+                    nc.tensor.matmul(
+                        out=pair[:, i * BANK : (i + 1) * BANK], lhsT=ones[:],
+                        rhs=bias_rows[:, b, cols], start=True, stop=True,
+                    )
+                return
             acc = acc_pool.tile([P, SPAN * BANK], F32, name="acc")
             spans[job] = acc
-            progress["open"] += 1
             for i in range(SPAN):
                 part = acc[:, i * BANK : (i + 1) * BANK]
-                if kind == "bias":
-                    b, n = job[1], job[2] * SPAN + i
-                    nc.tensor.matmul(
-                        out=part, lhsT=ones[:], rhs=bias_rows[:, b, n * BANK : (n + 1) * BANK],
-                        start=True, stop=True,
+                m, b, n = job[1], job[2], job[3] * SPAN + i
+                codes, plane = packed_of[m][b]
+                for g in range(PASSES):
+                    nc.tensor.matmul_mx(
+                        out=part,
+                        lhsT=codes[:, g * P : (g + 1) * P].bitcast(FP8X4),
+                        lhsT_scale=plane[:, g * P : (g + 1) * P],
+                        rhs=w_words[:, b, g, n * 2 * BANK : (n + 1) * 2 * BANK].bitcast(FP4X4),
+                        rhs_scale=w_planes[:, b, g, n * BANK : (n + 1) * BANK],
+                        start=(g == 0),
+                        stop=(g == PASSES - 1),
                     )
-                else:
-                    m, b, n = job[1], job[2], job[3] * SPAN + i
-                    codes, plane = packed_of[m][b]
-                    for g in range(PASSES):
-                        nc.tensor.matmul_mx(
-                            out=part,
-                            lhsT=codes[:, g * P : (g + 1) * P].bitcast(FP8X4),
-                            lhsT_scale=plane[:, g * P : (g + 1) * P],
-                            rhs=w_words[:, b, g, n * 2 * BANK : (n + 1) * 2 * BANK].bitcast(FP4X4),
-                            rhs_scale=w_planes[:, b, g, n * BANK : (n + 1) * BANK],
-                            start=(g == 0),
-                            stop=(g == PASSES - 1),
-                        )
 
         jobs = []
-        jobs.extend([("bias", 0, s) for s in range(SPANS)])
+        jobs.extend([("bias", 0, half) for half in range(2)])
         jobs.extend([("mm", 0, 0, s) for s in range(SPANS)])
-        jobs.extend([("bias", 1, s) for s in range(SPANS)])
+        jobs.extend([("bias", 1, half) for half in range(2)])
         jobs.append(("turn", 1))
         jobs.extend([("mm", 0, 1, s) for s in range(SPANS)])
         jobs.append(("turn", 2))
@@ -202,16 +207,13 @@ def tile_layernormgrucell_pa_kernel(
                 tensor_job(job)
                 progress["next"] += 1
 
-        def copy_bias(b, s, on_vector):
-            acc = spans[("bias", b, s)]
-            for i in range(SPAN):
-                n = s * SPAN + i
-                cols = slice(n * BANK, (n + 1) * BANK)
-                part = acc[:, i * BANK : (i + 1) * BANK]
-                if on_vector:
-                    nc.vector.tensor_copy(out=bias_all[:, b, cols], in_=part)
-                else:
-                    nc.scalar.copy(out=bias_all[:, b, cols], in_=part)
+        def copy_bias(b, half, on_vector):
+            pair = spans[("bias", b, half)]
+            cols = slice(half * HALF, (half + 1) * HALF)
+            if on_vector:
+                nc.vector.tensor_copy(out=bias_all[:, b, cols], in_=pair[:])
+            else:
+                nc.scalar.copy(out=bias_all[:, b, cols], in_=pair[:])
             progress["open"] -= 1
             fill()
 
@@ -325,8 +327,8 @@ def tile_layernormgrucell_pa_kernel(
         copy_turned(0)
         quantise(0)
         fill()
-        for s in range(SPANS):
-            copy_bias(0, s, s % 2 == 0)
+        for half in range(2):
+            copy_bias(0, half, half == 0)
         for m in range(ROW_TILES + LAG):
             if 0 < m <= ROW_TILES:
                 row_stats(m - 1, m < ROW_TILES)
@@ -336,8 +338,8 @@ def tile_layernormgrucell_pa_kernel(
             if m == 0:
                 copy_turned(1)
                 quantise(1)
-                for s in range(SPANS):
-                    copy_bias(1, s, s % 2 == 0)
+                for half in range(2):
+                    copy_bias(1, half, half == 0)
             if m < ROW_TILES:
                 if m + 2 < ROW_TILES:
                     copy_turned(m + 2)

@@ -65,11 +65,11 @@ def tile_layernormgrucell_pa_kernel(
         minus_half = keep.tile([P, BRANCHES], F32)
         warm = keep.tile([P, 1], F32)
 
+        nc.vector.memset(minus_half[:], -0.5)
         for b in range(BRANCHES):
             nc.vector.memset(bias_rows[:, b, :], 0.0)
             nc.vector.memset(w_planes[:, b, :, :].bitcast(I32), 0)
         nc.vector.memset(ones[:], 1.0)
-        nc.vector.memset(minus_half[:], -0.5)
         make_identity(nc, ident[:])
         nc.scalar.activation(out=warm[:], in_=minus_half[:, 0:1], func=ACT.Sigmoid)
 
@@ -98,7 +98,7 @@ def tile_layernormgrucell_pa_kernel(
 
         load_rows(0)
         for b in range(BRANCHES):
-            nc.scalar.dma_start(out=bias_rows[0:1, b, :], in_=biases[b].unsqueeze(0))
+            nc.gpsimd.dma_start(out=bias_rows[0:1, b, :], in_=biases[b].unsqueeze(0))
         load_scales(0)
         load_words(0)
         load_scales(1)

@@ -67,8 +67,9 @@ def tile_layernormgrucell_pa_kernel(
 
         nc.vector.memset(minus_half[:], -0.5)
         for b in range(BRANCHES):
-            nc.vector.memset(bias_rows[:, b, :], 0.0)
             nc.vector.memset(w_planes[:, b, :, :].bitcast(I32), 0)
+        for b in range(BRANCHES):
+            nc.vector.memset(bias_rows[:, b, :], 0.0)
         nc.vector.memset(ones[:], 1.0)
         make_identity(nc, ident[:])
         nc.scalar.activation(out=warm[:], in_=minus_half[:, 0:1], func=ACT.Sigmoid)
@@ -99,9 +100,9 @@ def tile_layernormgrucell_pa_kernel(
         load_rows(0)
         for b in range(BRANCHES):
             nc.gpsimd.dma_start(out=bias_rows[0:1, b, :], in_=biases[b].unsqueeze(0))
-        load_scales(0)
+        for b in range(BRANCHES):
+            load_scales(b)
         load_words(0)
-        load_scales(1)
         load_rows(1)
         load_words(1)
         for m in range(2, ROW_TILES):

@@ -25,10 +25,11 @@ PASSES = K // K_PASS
 BANK = 512
 BANKS = GATES // BANK
 HALVES = 2
+GROUPS = ((0, 1, 2, 3), (4, 5, 6), (7,))
 STORE_CHUNKS = 2
 HALF = 1024
 FIRST = 512
-LAG = 2
+LAG = 4
 LAST_CHUNKS = 2
 SPAN = 1
 SPANS = BANKS // SPAN
@@ -50,6 +51,7 @@ def tile_layernormgrucell_pa_kernel(
         keep = ctx.enter_context(tc.tile_pool(name="keep", bufs=1))
         stage = ctx.enter_context(tc.tile_pool(name="stage", bufs=2))
         rows3 = ctx.enter_context(tc.tile_pool(name="rows3", bufs=3))
+        rows8 = ctx.enter_context(tc.tile_pool(name="rows8", bufs=ROW_TILES))
         small = ctx.enter_context(tc.tile_pool(name="small", bufs=4))
         acc_pool = ctx.enter_context(tc.psum_pool(name="acc", bufs=ACC_SPANS))
         turn_pool = ctx.enter_context(tc.psum_pool(name="turn", bufs=2))
@@ -58,20 +60,19 @@ def tile_layernormgrucell_pa_kernel(
         raw = keep.tile([P, BRANCHES, ROW_TILES, K], BF16)
         w_words = keep.tile([P, BRANCHES, PASSES, 2 * GATES], U8, align_bytes=64)
         w_planes = keep.tile([P, BRANCHES, PASSES, GATES], U8, align_bytes=64)
-        bias_rows = keep.tile([P, BRANCHES, GATES], BF16)
+        bias_rows = keep.tile([P, BRANCHES, P], BF16)
         bias_all = keep.tile([P, BRANCHES, GATES], BF16)
-        ones = keep.tile([P, P], BF16)
         ident = keep.tile([P, P], F32)
-        minus_half = keep.tile([P, BRANCHES], F32)
+        pick = keep.tile([P, P], BF16)
+        minus_half = keep.tile([P, 4 * BRANCHES], F32)
         warm = keep.tile([P, 1], F32)
 
         nc.vector.memset(minus_half[:], -0.5)
+        nc.vector.memset(bias_rows[:], 0.0)
         for b in range(BRANCHES):
             nc.vector.memset(w_planes[:, b, :, :].bitcast(I32), 0)
-        for b in range(BRANCHES):
-            nc.vector.memset(bias_rows[:, b, :], 0.0)
-        nc.vector.memset(ones[:], 1.0)
         make_identity(nc, ident[:])
+        nc.vector.tensor_copy(out=pick[:], in_=ident[:])
         nc.scalar.activation(out=warm[:], in_=minus_half[:, 0:1], func=ACT.Sigmoid)
 
         def load_rows(m):
@@ -99,7 +100,9 @@ def tile_layernormgrucell_pa_kernel(
 
         load_rows(0)
         for b in range(BRANCHES):
-            nc.gpsimd.dma_start(out=bias_rows[0:1, b, :], in_=biases[b].unsqueeze(0))
+            nc.gpsimd.dma_start(
+                out=bias_rows[0 : GATES // P, b, :], in_=biases[b].rearrange("(k c) -> k c", c=P)
+            )
         for b in range(BRANCHES):
             load_scales(b)
         load_words(0)
@@ -111,6 +114,8 @@ def tile_layernormgrucell_pa_kernel(
         turned_of = {}
         sides_of = {}
         packed_of = {}
+        group_of = {m: group for group in GROUPS for m in group}
+        sums_of = {}
         rows_of = {}
         spans = {}
         progress = {"next": 0, "open": 0}
@@ -163,11 +168,12 @@ def tile_layernormgrucell_pa_kernel(
                 b, half = job[1], job[2]
                 pair = acc_pool.tile([P, HALF], BF16, name="acc")
                 spans[job] = pair
-                for i in range(HALF // BANK):
-                    cols = slice(half * HALF + i * BANK, half * HALF + (i + 1) * BANK)
+                for i in range(HALF // P):
+                    k = half * HALF // P + i
                     nc.tensor.matmul(
-                        out=pair[:, i * BANK : (i + 1) * BANK], lhsT=ones[:],
-                        rhs=bias_rows[:, b, cols], start=True, stop=True,
+                        out=pair[:, i * P : (i + 1) * P],
+                        lhsT=pick[:, k : k + 1].to_broadcast([P, P]),
+                        rhs=bias_rows[:, b, :], start=True, stop=True,
                     )
                 return
             acc = acc_pool.tile([P, SPAN * BANK], F32, name="acc")
@@ -188,8 +194,9 @@ def tile_layernormgrucell_pa_kernel(
                     )
 
         jobs = []
-        jobs.extend([("bias", 0, half) for half in range(2)])
-        jobs.extend([("mm", 0, 0, s) for s in range(SPANS)])
+        for half in range(2):
+            jobs.append(("bias", 0, half))
+            jobs.extend([("mm", 0, 0, s) for s in (2 * half, 2 * half + 1)])
         jobs.extend([("bias", 1, half) for half in range(2)])
         jobs.append(("turn", 1))
         jobs.extend([("mm", 0, 1, s) for s in range(SPANS)])
@@ -205,6 +212,8 @@ def tile_layernormgrucell_pa_kernel(
                 job = jobs[progress["next"]]
                 if job[0] != "turn" and progress["open"] >= ACC_SPANS:
                     break
+                if job[0] == "mm" and job[1] not in packed_of:
+                    break
                 tensor_job(job)
                 progress["next"] += 1
 
@@ -219,14 +228,24 @@ def tile_layernormgrucell_pa_kernel(
             fill()
 
         def start_rows(m):
+            group = group_of[m]
+            if m == group[0]:
+                width = len(group) * BRANCHES
+                sums_of[group] = (
+                    small.tile([P, width, SPANS], F32, name="sums"),
+                    small.tile([P, width], F32, name="sum_sq"),
+                )
+            sums, sum_sq = sums_of[group]
             rows_of[m] = {
-                "v": rows3.tile([P, BRANCHES, GATES], F32, name="v"),
-                "sum_sq": small.tile([P, BRANCHES], F32, name="sum_sq"),
-                "sums": small.tile([P, BRANCHES, SPANS], F32, name="sums"),
+                "v": rows8.tile([P, BRANCHES, GATES], F32, name="v"),
+                "sums": sums,
+                "sum_sq": sum_sq,
+                "first": (m - group[0]) * BRANCHES,
             }
 
-        def evacuate(m, b):
+        def evacuate(m, b, between=()):
             row = rows_of[m]
+            between = list(between)
             for s in range(SPANS):
                 cols = slice(s * SPAN * BANK, (s + 1) * SPAN * BANK)
                 nc.vector.scalar_tensor_tensor(
@@ -236,91 +255,101 @@ def tile_layernormgrucell_pa_kernel(
                     in1=bias_all[:, b, cols],
                     op0=ALU.mult,
                     op1=ALU.add,
-                    accum_out=row["sums"][:, b, s : s + 1],
+                    accum_out=row["sums"][:, row["first"] + b, s : s + 1],
                 )
                 progress["open"] -= 1
                 fill()
+                if between:
+                    between.pop(0)()
 
         def square(m, b):
             row = rows_of[m]
+            j = row["first"] + b
             squares = stage.tile([P, GATES], BF16, name="squares")
             nc.scalar.activation(
                 out=squares[:],
                 in_=row["v"][:, b, :],
                 func=ACT.Square,
-                bias=row["sums"][:, b, 0:1],
+                bias=row["sums"][:, j, 0:1],
                 scale=-float(FIRST),
-                accum_out=row["sum_sq"][:, b : b + 1],
+                accum_out=row["sum_sq"][:, j : j + 1],
             )
 
-        def row_stats(m, squares_first):
-            row = rows_of[m]
-            sums = row["sums"]
-            raw_eps = small.tile([P, BRANCHES], F32, name="raw_eps")
-            pairs = small.tile([P, BRANCHES, 2], F32, name="pairs")
-            total = small.tile([P, BRANCHES], F32, name="total")
-            neg_mean = small.tile([P, BRANCHES], F32, name="neg_mean")
-            neg_centre = small.tile([P, BRANCHES], F32, name="neg_centre")
-            off = small.tile([P, BRANCHES], F32, name="off")
-            off_sq = small.tile([P, BRANCHES], F32, name="off_sq")
-            var_eps = small.tile([P, BRANCHES], F32, name="var_eps")
-            rstd = small.tile([P, BRANCHES], F32, name="rstd")
-            ratio = small.tile([P, 1], F32, name="ratio")
-            parts = small.tile([P, BRANCHES], F32, name="parts")
-            shift = small.tile([P, 1], F32, name="shift")
-
-            def from_squares():
-                nc.gpsimd.tensor_scalar(
-                    out=raw_eps[:], in0=row["sum_sq"][:], scalar1=1.0 / (GATES * FIRST * FIRST),
+        def row_stats(group):
+            sums, sum_sq = sums_of[group]
+            count = len(group)
+            width = count * BRANCHES
+            total = small.tile([P, width], F32, name="total")
+            raw_eps = small.tile([P, width], F32, name="raw_eps")
+            off = small.tile([P, width], F32, name="off")
+            off_sq = small.tile([P, width], F32, name="off_sq")
+            var_eps = small.tile([P, width], F32, name="var_eps")
+            rstd = small.tile([P, width], F32, name="rstd")
+            parts = small.tile([P, width], F32, name="parts")
+            shift = small.tile([P, count], F32, name="shift")
+            prod = small.tile([P, count], F32, name="prod")
+            ratio = small.tile([P, count], F32, name="ratio")
+            for i, m in enumerate(group):
+                rows_of[m]["ratio"] = ratio[:, i : i + 1]
+                rows_of[m]["shift"] = shift[:, i : i + 1]
+                rows_of[m]["scale"] = rstd[:, i * BRANCHES : i * BRANCHES + 1]
+            variance = (
+                lambda: nc.vector.tensor_reduce(
+                    out=total[:], in_=sums[:], op=ALU.add, axis=mybir.AxisListType.X
+                ),
+                lambda: nc.vector.scalar_tensor_tensor(
+                    out=off[:], in0=sums[:, :, 0], scalar=-float(GATES // FIRST), in1=total[:],
+                    op0=ALU.mult, op1=ALU.add,
+                ),
+                lambda: nc.vector.scalar_tensor_tensor(
+                    out=off_sq[:], in0=off[:], scalar=1.0 / GATES**2, in1=off[:],
+                    op0=ALU.mult, op1=ALU.mult,
+                ),
+                lambda: nc.vector.tensor_scalar(
+                    out=raw_eps[:], in0=sum_sq[:], scalar1=1.0 / (GATES * FIRST * FIRST),
                     scalar2=EPS, op0=ALU.mult, op1=ALU.add,
+                ),
+                lambda: nc.vector.tensor_tensor(
+                    out=var_eps[:], in0=raw_eps[:], in1=off_sq[:], op=ALU.subtract
+                ),
+            )
+
+            def power():
+                nc.gpsimd.tensor_tensor(
+                    out=rstd[:], in0=var_eps[:], in1=minus_half[:, 0:width], op=ALU.pow
                 )
 
-            if squares_first:
-                from_squares()
-            nc.gpsimd.tensor_tensor(
-                out=pairs[:], in0=sums[:, :, 0:2], in1=sums[:, :, 2:4], op=ALU.add
+            factors = (
+                lambda: nc.vector.tensor_tensor(
+                    out=prod[:], in0=rstd[:, 0::BRANCHES], in1=rstd[:, 1::BRANCHES], op=ALU.mult
+                ),
+                lambda: nc.vector.scalar_tensor_tensor(
+                    out=parts[:], in0=rstd[:], scalar=-1.0 / GATES, in1=total[:],
+                    op0=ALU.mult, op1=ALU.mult,
+                ),
+                lambda: nc.vector.tensor_tensor(
+                    out=ratio[:], in0=var_eps[:, 0::BRANCHES], in1=prod[:], op=ALU.mult
+                ),
+                lambda: nc.vector.tensor_tensor(
+                    out=shift[:], in0=parts[:, 0::BRANCHES], in1=parts[:, 1::BRANCHES], op=ALU.add
+                ),
             )
-            nc.gpsimd.tensor_tensor(
-                out=total[:], in0=pairs[:, :, 0], in1=pairs[:, :, 1], op=ALU.add
-            )
-            nc.gpsimd.tensor_scalar(
-                out=neg_mean[:], in0=total[:], scalar1=-1.0 / GATES, scalar2=0.0,
-                op0=ALU.mult, op1=ALU.add,
-            )
-            nc.gpsimd.tensor_scalar(
-                out=neg_centre[:], in0=sums[:, :, 0], scalar1=-1.0 / FIRST, scalar2=0.0,
-                op0=ALU.mult, op1=ALU.add,
-            )
-            nc.gpsimd.tensor_tensor(out=off[:], in0=neg_mean[:], in1=neg_centre[:], op=ALU.subtract)
-            nc.gpsimd.tensor_tensor(out=off_sq[:], in0=off[:], in1=off[:], op=ALU.mult)
-            if not squares_first:
-                from_squares()
-            nc.gpsimd.tensor_tensor(out=var_eps[:], in0=raw_eps[:], in1=off_sq[:], op=ALU.subtract)
-            nc.gpsimd.tensor_tensor(out=rstd[:], in0=var_eps[:], in1=minus_half[:], op=ALU.pow)
-            nc.gpsimd.tensor_scalar(
-                out=ratio[:], in0=var_eps[:, 0:1], scalar1=rstd[:, 0:1], scalar2=rstd[:, 1:2],
-                op0=ALU.mult, op1=ALU.mult,
-            )
-            nc.gpsimd.tensor_tensor(out=parts[:], in0=rstd[:], in1=neg_mean[:], op=ALU.mult)
-            nc.gpsimd.tensor_tensor(out=shift[:], in0=parts[:, 0:1], in1=parts[:, 1:2], op=ALU.add)
-            row["rstd"] = rstd
-            row["ratio"] = ratio
-            row["shift"] = shift
+            return variance, power, factors
 
         def finish(m, chunks):
             row = rows_of[m]
-            gate = rows3.tile([P, GATES], F32, name="gate")
             v = row["v"]
+            gate = v[:, 0, :]
             width = GATES // chunks
             for c in range(chunks):
                 cols = slice(c * width, (c + 1) * width)
                 nc.vector.scalar_tensor_tensor(
-                    out=gate[:, cols], in0=v[:, 1, cols], scalar=row["ratio"][:, 0:1],
+                    out=gate[:, cols], in0=v[:, 1, cols], scalar=row["ratio"],
                     in1=v[:, 0, cols], op0=ALU.mult, op1=ALU.add,
                 )
                 nc.scalar.activation(
                     out=gate[:, cols], in_=gate[:, cols], func=ACT.Sigmoid,
-                    bias=row["shift"][:, 0:1], scale=row["rstd"][:, 0:1],
+                    bias=row["shift"], scale=row["scale"],
                 )
                 nc.sync.dma_start(out=out[m * P : (m + 1) * P, cols], in_=gate[:, cols])
 
@@ -330,24 +359,35 @@ def tile_layernormgrucell_pa_kernel(
         fill()
         for half in range(2):
             copy_bias(0, half, half == 0)
-        for m in range(ROW_TILES + LAG):
-            if 0 < m <= ROW_TILES:
-                row_stats(m - 1, m < ROW_TILES)
-            if m < ROW_TILES:
-                start_rows(m)
-                evacuate(m, 0)
+        for m in range(ROW_TILES):
+            start_rows(m)
+            ended = [group for group in GROUPS if group[-1] == m - 1]
+            variance, power, factors = row_stats(ended[0]) if ended else ((), None, ())
+            evacuate(m, 0, variance[0:3])
             if m == 0:
                 copy_turned(1)
-                quantise(1)
+            if m + 1 < ROW_TILES:
+                quantise(m + 1)
+                fill()
+            if m == 0:
                 for half in range(2):
                     copy_bias(1, half, half == 0)
-            if m < ROW_TILES:
-                if m + 2 < ROW_TILES:
-                    copy_turned(m + 2)
-                square(m, 0)
-                evacuate(m, 1)
-                square(m, 1)
-                if m + 2 < ROW_TILES:
-                    quantise(m + 2)
+            square(m, 0)
+            if m + 2 < ROW_TILES:
+                copy_turned(m + 2)
+            evacuate(m, 1, (*variance[3:5], power) if ended else ())
+            square(m, 1)
+            for step in factors:
+                step()
             if m >= LAG:
-                finish(m - LAG, STORE_CHUNKS if m - LAG < ROW_TILES - 1 else LAST_CHUNKS)
+                finish(m - LAG, STORE_CHUNKS)
+        variance, power, factors = row_stats(GROUPS[-1])
+        finish(ROW_TILES - 4, STORE_CHUNKS)
+        for step in variance:
+            step()
+        power()
+        finish(ROW_TILES - 3, STORE_CHUNKS)
+        for step in factors:
+            step()
+        finish(ROW_TILES - 2, STORE_CHUNKS)
+        finish(ROW_TILES - 1, LAST_CHUNKS)

@@ -194,10 +194,8 @@ def tile_layernormgrucell_pa_kernel(
                     )
 
         jobs = []
-        for half in range(2):
-            jobs.append(("bias", 0, half))
-            jobs.extend([("mm", 0, 0, s) for s in (2 * half, 2 * half + 1)])
-        jobs.extend([("bias", 1, half) for half in range(2)])
+        jobs.extend([("bias", b, half) for b in range(BRANCHES) for half in range(2)])
+        jobs.extend([("mm", 0, 0, s) for s in range(SPANS)])
         jobs.append(("turn", 1))
         jobs.extend([("mm", 0, 1, s) for s in range(SPANS)])
         jobs.append(("turn", 2))
@@ -357,37 +355,45 @@ def tile_layernormgrucell_pa_kernel(
         copy_turned(0)
         quantise(0)
         fill()
-        for half in range(2):
-            copy_bias(0, half, half == 0)
+        for b in range(BRANCHES):
+            for half in range(2):
+                copy_bias(b, half, True)
+
+        def chunks_of(m):
+            return STORE_CHUNKS if m >= ROW_TILES - 2 else 2
+
         for m in range(ROW_TILES):
             start_rows(m)
             ended = [group for group in GROUPS if group[-1] == m - 1]
             variance, power, factors = row_stats(ended[0]) if ended else ((), None, ())
+            waits = bool(ended) and m - LAG in ended[0]
             evacuate(m, 0, variance[0:3])
             if m == 0:
                 copy_turned(1)
-            if m + 1 < ROW_TILES:
+            if m + 1 < ROW_TILES and not waits:
                 quantise(m + 1)
                 fill()
-            if m == 0:
-                for half in range(2):
-                    copy_bias(1, half, half == 0)
             square(m, 0)
             if m + 2 < ROW_TILES:
                 copy_turned(m + 2)
             evacuate(m, 1, (*variance[3:5], power) if ended else ())
             square(m, 1)
+            if m + 1 < ROW_TILES and waits:
+                quantise(m + 1)
+                fill()
+            if ended and not waits and m >= LAG:
+                finish(m - LAG, chunks_of(m - LAG))
             for step in factors:
                 step()
-            if m >= LAG:
-                finish(m - LAG, STORE_CHUNKS)
+            if m >= LAG and (waits or not ended):
+                finish(m - LAG, chunks_of(m - LAG))
         variance, power, factors = row_stats(GROUPS[-1])
-        finish(ROW_TILES - 4, STORE_CHUNKS)
-        for step in variance:
-            step()
-        power()
-        finish(ROW_TILES - 3, STORE_CHUNKS)
-        for step in factors:
-            step()
-        finish(ROW_TILES - 2, STORE_CHUNKS)
-        finish(ROW_TILES - 1, LAST_CHUNKS)
+        for i, m in enumerate(range(ROW_TILES - LAG, ROW_TILES)):
+            finish(m, chunks_of(m))
+            if i == 0:
+                for step in variance:
+                    step()
+                power()
+            if i == 1:
+                for step in factors:
+                    step()

@@ -58,8 +58,18 @@ def tile_layernormgrucell_pa_kernel(
         ctx.enter_context(tc.manual_schedule())
 
         raw = keep.tile([P, BRANCHES, ROW_TILES, K], BF16)
-        w_words = keep.tile([P, BRANCHES, PASSES, 2 * GATES], U8, align_bytes=64)
-        w_planes = keep.tile([P, BRANCHES, PASSES, GATES], U8, align_bytes=64)
+        w_words = []
+        w_planes = []
+        for b in range(BRANCHES):
+            plane = keep.tile([P, PASSES, GATES], U8, align_bytes=64, name="w_plane%d" % b)
+            w_planes.append(plane)
+            banks = []
+            for n in range(BANKS):
+                words = keep.tile(
+                    [P, PASSES, 2 * BANK], U8, align_bytes=64, name="words%d_%d" % (b, n)
+                )
+                banks.append(words)
+            w_words.append(banks)
         bias_rows = keep.tile([P, BRANCHES, P], BF16)
         bias_all = keep.tile([P, BRANCHES, GATES], BF16)
         ident = keep.tile([P, P], F32)
@@ -70,43 +80,41 @@ def tile_layernormgrucell_pa_kernel(
         nc.vector.memset(minus_half[:], -0.5)
         nc.vector.memset(bias_rows[:], 0.0)
         for b in range(BRANCHES):
-            nc.vector.memset(w_planes[:, b, :, :].bitcast(I32), 0)
+            nc.vector.memset(w_planes[b][:].bitcast(I32), 0)
         make_identity(nc, ident[:])
         nc.vector.tensor_copy(out=pick[:], in_=ident[:])
-        nc.scalar.activation(out=warm[:], in_=minus_half[:, 0:1], func=ACT.Sigmoid)
-
         def load_rows(m):
             for b in range(BRANCHES):
                 nc.sync.dma_start(out=raw[:, b, m, :], in_=acts[b][m * P : (m + 1) * P, :])
 
         def load_scales(b):
-            planes = w_planes[:].bitcast(I32)
+            planes = w_planes[b][:].bitcast(I32)
             rows = weight_scales[b].bitcast(I32)
             for r in range(4):
                 nc.sync.dma_start(
-                    out=planes[r : P : 32, b, :, :],
+                    out=planes[r : P : 32, :, :],
                     in_=rows[:, r : 16 : 4, :].rearrange("g q c -> q g c"),
                 )
 
         def load_words(b):
-            words = w_words[:].bitcast(I32)
             source = weight_words[b].bitcast(I32)
             step = 2 * BANK // 4
             for n in range(BANKS):
                 nc.sync.dma_start(
-                    out=words[:, b, :, n * step : (n + 1) * step],
+                    out=w_words[b][n][:].bitcast(I32),
                     in_=source[:, :, n * step : (n + 1) * step].rearrange("g p c -> p g c"),
                 )
 
-        load_rows(0)
-        for b in range(BRANCHES):
-            nc.gpsimd.dma_start(
+        for b, queue in enumerate((nc.scalar, nc.gpsimd)):
+            queue.dma_start(
                 out=bias_rows[0 : GATES // P, b, :], in_=biases[b].rearrange("(k c) -> k c", c=P)
             )
-        for b in range(BRANCHES):
-            load_scales(b)
+        nc.scalar.activation(out=warm[:], in_=minus_half[:, 0:1], func=ACT.Sigmoid)
+        load_rows(0)
+        load_scales(0)
         load_words(0)
         load_rows(1)
+        load_scales(1)
         load_words(1)
         for m in range(2, ROW_TILES):
             load_rows(m)
@@ -137,26 +145,32 @@ def tile_layernormgrucell_pa_kernel(
             turned_of[m] = both
 
         def copy_turned(m):
-            sides = []
+            side = stage.tile([P, BRANCHES, PASSES * P * 4], BF16, align_bytes=64, name="side")
             for b in range(BRANCHES):
-                side = stage.tile([P, PASSES * P * 4], BF16, align_bytes=64, name="side%d" % b)
                 nc.scalar.copy(
-                    out=side[:].bitcast(F32).rearrange("p (g r u) -> p g r u", g=PASSES, u=HALVES),
+                    out=side[:, b, :].bitcast(F32).rearrange(
+                        "p (g r u) -> p g r u", g=PASSES, u=HALVES
+                    ),
                     in_=turned_of[m][b][:].rearrange("p (g u) r -> p g r u", u=HALVES),
                 )
-                sides.append(side)
-            sides_of[m] = sides
+            sides_of[m] = side
 
         def quantise(m):
-            packed = []
-            for b in range(BRANCHES):
-                codes = rows3.tile([P, PASSES * P], U32, align_bytes=64, name="codes%d" % b)
-                plane = rows3.tile([P, PASSES * P], U8, align_bytes=64, name="plane%d" % b)
+            codes = rows3.tile([P, BRANCHES, PASSES * P], U32, align_bytes=64, name="codes")
+            plane = rows3.tile([P, BRANCHES, PASSES * P], U8, align_bytes=64, name="plane")
+            side = sides_of[m]
+            if m == 0:
+                for b in range(BRANCHES):
+                    nc.vector.quantize_mx(
+                        out=codes[:, b, :].bitcast(FP8X4), scales=plane[:, b, :], in_=side[:, b, :]
+                    )
+            else:
                 nc.vector.quantize_mx(
-                    out=codes[:].bitcast(FP8X4), scales=plane[:], in_=sides_of[m][b][:]
+                    out=codes[:].rearrange("p b w -> p (b w)").bitcast(FP8X4),
+                    scales=plane[:].rearrange("p b w -> p (b w)"),
+                    in_=side[:].rearrange("p b k -> p (b k)"),
                 )
-                packed.append((codes, plane))
-            packed_of[m] = packed
+            packed_of[m] = (codes, plane)
 
         def tensor_job(job):
             kind = job[0]
@@ -181,22 +195,22 @@ def tile_layernormgrucell_pa_kernel(
             for i in range(SPAN):
                 part = acc[:, i * BANK : (i + 1) * BANK]
                 m, b, n = job[1], job[2], job[3] * SPAN + i
-                codes, plane = packed_of[m][b]
+                codes, plane = packed_of[m]
                 for g in range(PASSES):
                     nc.tensor.matmul_mx(
                         out=part,
-                        lhsT=codes[:, g * P : (g + 1) * P].bitcast(FP8X4),
-                        lhsT_scale=plane[:, g * P : (g + 1) * P],
-                        rhs=w_words[:, b, g, n * 2 * BANK : (n + 1) * 2 * BANK].bitcast(FP4X4),
-                        rhs_scale=w_planes[:, b, g, n * BANK : (n + 1) * BANK],
+                        lhsT=codes[:, b, g * P : (g + 1) * P].bitcast(FP8X4),
+                        lhsT_scale=plane[:, b, g * P : (g + 1) * P],
+                        rhs=w_words[b][n][:, g, :].bitcast(FP4X4),
+                        rhs_scale=w_planes[b][:, g, n * BANK : (n + 1) * BANK],
                         start=(g == 0),
                         stop=(g == PASSES - 1),
                     )
 
         jobs = []
-        jobs.extend([("bias", b, half) for b in range(BRANCHES) for half in range(2)])
+        jobs.extend([("bias", 0, 0), ("bias", 0, 1), ("bias", 1, 0)])
         jobs.extend([("mm", 0, 0, s) for s in range(SPANS)])
-        jobs.append(("turn", 1))
+        jobs.extend([("turn", 1), ("bias", 1, 1)])
         jobs.extend([("mm", 0, 1, s) for s in range(SPANS)])
         jobs.append(("turn", 2))
         for m in range(1, ROW_TILES):
@@ -355,9 +369,9 @@ def tile_layernormgrucell_pa_kernel(
         copy_turned(0)
         quantise(0)
         fill()
-        for b in range(BRANCHES):
-            for half in range(2):
-                copy_bias(b, half, True)
+        copy_bias(0, 0, True)
+        copy_bias(0, 1, True)
+        copy_bias(1, 0, True)
 
         def chunks_of(m):
             return STORE_CHUNKS if m >= ROW_TILES - 2 else 2
@@ -369,6 +383,7 @@ def tile_layernormgrucell_pa_kernel(
             waits = bool(ended) and m - LAG in ended[0]
             evacuate(m, 0, variance[0:3])
             if m == 0:
+                copy_bias(1, 1, True)
                 copy_turned(1)
             if m + 1 < ROW_TILES and not waits:
                 quantise(m + 1)

from contextlib import ExitStack

import concourse.mybir as mybir
from concourse.masks import make_identity

F32 = mybir.dt.float32
BF16 = mybir.dt.bfloat16
I32 = mybir.dt.int32
U32 = mybir.dt.uint32
U8 = mybir.dt.uint8
FP8X4 = mybir.dt.float8_e4m3fn_x4
FP4X4 = mybir.dt.float4_e2m1fn_x4
ALU = mybir.AluOpType
ACT = mybir.ActivationFunctionType

P = 128
ROWS = 1024
K = 1024
GATES = 2048
EPS = 1e-5
BRANCHES = 2
ROW_TILES = ROWS // P
K_PASS = 4 * P
PASSES = K // K_PASS
BANK = 512
BANKS = GATES // BANK
HALVES = 2
GROUPS = ((0, 1, 2, 3), (4, 5, 6), (7,))
STORE_CHUNKS = 2
HALF = 1024
FIRST = 512
LAG = 4
LAST_CHUNKS = 2
SPAN = 1
SPANS = BANKS // SPAN
ACC_SPANS = 6 // SPAN

FLOPS = 2 * BRANCHES * ROWS * K * GATES


def tile_layernormgrucell_pa_kernel(
    tc, x, h, W_irz_words, W_irz_scales, b_irz, W_hrz_words, W_hrz_scales, b_hrz, out
):
    nc = tc.nc
    acts = (x, h)
    weight_words = (W_irz_words, W_hrz_words)
    weight_scales = (W_irz_scales, W_hrz_scales)
    biases = (b_irz, b_hrz)

    with ExitStack() as ctx:
        keep = ctx.enter_context(tc.tile_pool(name="keep", bufs=1))
        stage = ctx.enter_context(tc.tile_pool(name="stage", bufs=2))
        rows3 = ctx.enter_context(tc.tile_pool(name="rows3", bufs=3))
        rows8 = ctx.enter_context(tc.tile_pool(name="rows8", bufs=ROW_TILES))
        small = ctx.enter_context(tc.tile_pool(name="small", bufs=4))
        acc_pool = ctx.enter_context(tc.psum_pool(name="acc", bufs=ACC_SPANS))
        turn_pool = ctx.enter_context(tc.psum_pool(name="turn", bufs=2))
        ctx.enter_context(tc.manual_schedule())

        raw = keep.tile([P, BRANCHES, ROW_TILES, K], BF16)
        w_words = []
        w_planes = []
        for b in range(BRANCHES):
            plane = keep.tile([P, PASSES, GATES], U8, align_bytes=64, name="w_plane%d" % b)
            w_planes.append(plane)
            banks = []
            for n in range(BANKS):
                words = keep.tile(
                    [P, PASSES, 2 * BANK], U8, align_bytes=64, name="words%d_%d" % (b, n)
                )
                banks.append(words)
            w_words.append(banks)
        bias_rows = keep.tile([P, BRANCHES, P], BF16)
        bias_all = keep.tile([P, BRANCHES, GATES], BF16)
        ident = keep.tile([P, P], F32)
        pick = keep.tile([P, P], BF16)
        minus_half = keep.tile([P, 4 * BRANCHES], F32)
        warm = keep.tile([P, 1], F32)

        nc.vector.memset(minus_half[:], -0.5)
        nc.vector.memset(bias_rows[:], 0.0)
        for b in range(BRANCHES):
            nc.vector.memset(w_planes[b][:].bitcast(I32), 0)
        make_identity(nc, ident[:])
        nc.vector.tensor_copy(out=pick[:], in_=ident[:])
        def load_rows(m):
            for b in range(BRANCHES):
                nc.sync.dma_start(out=raw[:, b, m, :], in_=acts[b][m * P : (m + 1) * P, :])

        def load_scales(b):
            planes = w_planes[b][:].bitcast(I32)
            rows = weight_scales[b].bitcast(I32)
            for r in range(4):
                nc.sync.dma_start(
                    out=planes[r : P : 32, :, :],
                    in_=rows[:, r : 16 : 4, :].rearrange("g q c -> q g c"),
                )

        def load_words(b):
            source = weight_words[b].bitcast(I32)
            step = 2 * BANK // 4
            for n in range(BANKS):
                nc.sync.dma_start(
                    out=w_words[b][n][:].bitcast(I32),
                    in_=source[:, :, n * step : (n + 1) * step].rearrange("g p c -> p g c"),
                )

        for b, queue in enumerate((nc.scalar, nc.gpsimd)):
            queue.dma_start(
                out=bias_rows[0 : GATES // P, b, :], in_=biases[b].rearrange("(k c) -> k c", c=P)
            )
        nc.scalar.activation(out=warm[:], in_=minus_half[:, 0:1], func=ACT.Sigmoid)
        load_rows(0)
        load_scales(0)
        load_words(0)
        load_rows(1)
        load_scales(1)
        load_words(1)
        for m in range(2, ROW_TILES):
            load_rows(m)

        turned_of = {}
        sides_of = {}
        packed_of = {}
        group_of = {m: group for group in GROUPS for m in group}
        sums_of = {}
        rows_of = {}
        spans = {}
        progress = {"next": 0, "open": 0}

        def transposes(m):
            both = []
            for b in range(BRANCHES):
                words = raw[:, b, m, :].bitcast(F32)
                turned = turn_pool.tile([P, PASSES * HALVES, P], F32, name="turned")
                for g in range(PASSES):
                    for u in range(HALVES):
                        first = g * K_PASS // 2 + u
                        nc.tensor.transpose(
                            turned[:, g * HALVES + u, :],
                            words[:, first : (g + 1) * K_PASS // 2 : HALVES],
                            ident[:],
                        )
                both.append(turned)
            turned_of[m] = both

        def copy_turned(m):
            side = stage.tile([P, BRANCHES, PASSES * P * 4], BF16, align_bytes=64, name="side")
            for b in range(BRANCHES):
                nc.scalar.copy(
                    out=side[:, b, :].bitcast(F32).rearrange(
                        "p (g r u) -> p g r u", g=PASSES, u=HALVES
                    ),
                    in_=turned_of[m][b][:].rearrange("p (g u) r -> p g r u", u=HALVES),
                )
            sides_of[m] = side

        def quantise(m):
            codes = rows3.tile([P, BRANCHES, PASSES * P], U32, align_bytes=64, name="codes")
            plane = rows3.tile([P, BRANCHES, PASSES * P], U8, align_bytes=64, name="plane")
            side = sides_of[m]
            if m == 0:
                for b in range(BRANCHES):
                    nc.vector.quantize_mx(
                        out=codes[:, b, :].bitcast(FP8X4), scales=plane[:, b, :], in_=side[:, b, :]
                    )
            else:
                nc.vector.quantize_mx(
                    out=codes[:].rearrange("p b w -> p (b w)").bitcast(FP8X4),
                    scales=plane[:].rearrange("p b w -> p (b w)"),
                    in_=side[:].rearrange("p b k -> p (b k)"),
                )
            packed_of[m] = (codes, plane)

        def tensor_job(job):
            kind = job[0]
            if kind == "turn":
                transposes(job[1])
                return
            progress["open"] += 1
            if kind == "bias":
                b, half = job[1], job[2]
                pair = acc_pool.tile([P, HALF], BF16, name="acc")
                spans[job] = pair
                for i in range(HALF // P):
                    k = half * HALF // P + i
                    nc.tensor.matmul(
                        out=pair[:, i * P : (i + 1) * P],
                        lhsT=pick[:, k : k + 1].to_broadcast([P, P]),
                        rhs=bias_rows[:, b, :], start=True, stop=True,
                    )
                return
            acc = acc_pool.tile([P, SPAN * BANK], F32, name="acc")
            spans[job] = acc
            for i in range(SPAN):
                part = acc[:, i * BANK : (i + 1) * BANK]
                m, b, n = job[1], job[2], job[3] * SPAN + i
                codes, plane = packed_of[m]
                for g in range(PASSES):
                    nc.tensor.matmul_mx(
                        out=part,
                        lhsT=codes[:, b, g * P : (g + 1) * P].bitcast(FP8X4),
                        lhsT_scale=plane[:, b, g * P : (g + 1) * P],
                        rhs=w_words[b][n][:, g, :].bitcast(FP4X4),
                        rhs_scale=w_planes[b][:, g, n * BANK : (n + 1) * BANK],
                        start=(g == 0),
                        stop=(g == PASSES - 1),
                    )

        jobs = []
        jobs.extend([("bias", 0, 0), ("bias", 0, 1), ("bias", 1, 0)])
        jobs.extend([("mm", 0, 0, s) for s in range(SPANS)])
        jobs.extend([("turn", 1), ("bias", 1, 1)])
        jobs.extend([("mm", 0, 1, s) for s in range(SPANS)])
        jobs.append(("turn", 2))
        for m in range(1, ROW_TILES):
            for b in range(BRANCHES):
                jobs.extend([("mm", m, b, s) for s in range(SPANS)])
            if m + 2 < ROW_TILES:
                jobs.append(("turn", m + 2))

        def fill():
            while progress["next"] < len(jobs):
                job = jobs[progress["next"]]
                if job[0] != "turn" and progress["open"] >= ACC_SPANS:
                    break
                if job[0] == "mm" and job[1] not in packed_of:
                    break
                tensor_job(job)
                progress["next"] += 1

        def copy_bias(b, half, on_vector):
            pair = spans[("bias", b, half)]
            cols = slice(half * HALF, (half + 1) * HALF)
            if on_vector:
                nc.vector.tensor_copy(out=bias_all[:, b, cols], in_=pair[:])
            else:
                nc.scalar.copy(out=bias_all[:, b, cols], in_=pair[:])
            progress["open"] -= 1
            fill()

        def start_rows(m):
            group = group_of[m]
            if m == group[0]:
                width = len(group) * BRANCHES
                sums_of[group] = (
                    small.tile([P, width, SPANS], F32, name="sums"),
                    small.tile([P, width], F32, name="sum_sq"),
                )
            sums, sum_sq = sums_of[group]
            rows_of[m] = {
                "v": rows8.tile([P, BRANCHES, GATES], F32, name="v"),
                "sums": sums,
                "sum_sq": sum_sq,
                "first": (m - group[0]) * BRANCHES,
            }

        def evacuate(m, b, between=()):
            row = rows_of[m]
            between = list(between)
            for s in range(SPANS):
                cols = slice(s * SPAN * BANK, (s + 1) * SPAN * BANK)
                nc.vector.scalar_tensor_tensor(
                    out=row["v"][:, b, cols],
                    in0=spans[("mm", m, b, s)][:],
                    scalar=1.0,
                    in1=bias_all[:, b, cols],
                    op0=ALU.mult,
                    op1=ALU.add,
                    accum_out=row["sums"][:, row["first"] + b, s : s + 1],
                )
                progress["open"] -= 1
                fill()
                if between:
                    between.pop(0)()

        def square(m, b):
            row = rows_of[m]
            j = row["first"] + b
            squares = stage.tile([P, GATES], BF16, name="squares")
            nc.scalar.activation(
                out=squares[:],
                in_=row["v"][:, b, :],
                func=ACT.Square,
                bias=row["sums"][:, j, 0:1],
                scale=-float(FIRST),
                accum_out=row["sum_sq"][:, j : j + 1],
            )

        def row_stats(group):
            sums, sum_sq = sums_of[group]
            count = len(group)
            width = count * BRANCHES
            total = small.tile([P, width], F32, name="total")
            raw_eps = small.tile([P, width], F32, name="raw_eps")
            off = small.tile([P, width], F32, name="off")
            off_sq = small.tile([P, width], F32, name="off_sq")
            var_eps = small.tile([P, width], F32, name="var_eps")
            rstd = small.tile([P, width], F32, name="rstd")
            parts = small.tile([P, width], F32, name="parts")
            shift = small.tile([P, count], F32, name="shift")
            prod = small.tile([P, count], F32, name="prod")
            ratio = small.tile([P, count], F32, name="ratio")
            for i, m in enumerate(group):
                rows_of[m]["ratio"] = ratio[:, i : i + 1]
                rows_of[m]["shift"] = shift[:, i : i + 1]
                rows_of[m]["scale"] = rstd[:, i * BRANCHES : i * BRANCHES + 1]
            variance = (
                lambda: nc.vector.tensor_reduce(
                    out=total[:], in_=sums[:], op=ALU.add, axis=mybir.AxisListType.X
                ),
                lambda: nc.vector.scalar_tensor_tensor(
                    out=off[:], in0=sums[:, :, 0], scalar=-float(GATES // FIRST), in1=total[:],
                    op0=ALU.mult, op1=ALU.add,
                ),
                lambda: nc.vector.scalar_tensor_tensor(
                    out=off_sq[:], in0=off[:], scalar=1.0 / GATES**2, in1=off[:],
                    op0=ALU.mult, op1=ALU.mult,
                ),
                lambda: nc.vector.tensor_scalar(
                    out=raw_eps[:], in0=sum_sq[:], scalar1=1.0 / (GATES * FIRST * FIRST),
                    scalar2=EPS, op0=ALU.mult, op1=ALU.add,
                ),
                lambda: nc.vector.tensor_tensor(
                    out=var_eps[:], in0=raw_eps[:], in1=off_sq[:], op=ALU.subtract
                ),
            )

            def power():
                nc.gpsimd.tensor_tensor(
                    out=rstd[:], in0=var_eps[:], in1=minus_half[:, 0:width], op=ALU.pow
                )

            factors = (
                lambda: nc.vector.tensor_tensor(
                    out=prod[:], in0=rstd[:, 0::BRANCHES], in1=rstd[:, 1::BRANCHES], op=ALU.mult
                ),
                lambda: nc.vector.scalar_tensor_tensor(
                    out=parts[:], in0=rstd[:], scalar=-1.0 / GATES, in1=total[:],
                    op0=ALU.mult, op1=ALU.mult,
                ),
                lambda: nc.vector.tensor_tensor(
                    out=ratio[:], in0=var_eps[:, 0::BRANCHES], in1=prod[:], op=ALU.mult
                ),
                lambda: nc.vector.tensor_tensor(
                    out=shift[:], in0=parts[:, 0::BRANCHES], in1=parts[:, 1::BRANCHES], op=ALU.add
                ),
            )
            return variance, power, factors

        def finish(m, chunks):
            row = rows_of[m]
            v = row["v"]
            gate = v[:, 0, :]
            width = GATES // chunks
            for c in range(chunks):
                cols = slice(c * width, (c + 1) * width)
                nc.vector.scalar_tensor_tensor(
                    out=gate[:, cols], in0=v[:, 1, cols], scalar=row["ratio"],
                    in1=v[:, 0, cols], op0=ALU.mult, op1=ALU.add,
                )
                nc.scalar.activation(
                    out=gate[:, cols], in_=gate[:, cols], func=ACT.Sigmoid,
                    bias=row["shift"], scale=row["scale"],
                )
                nc.sync.dma_start(out=out[m * P : (m + 1) * P, cols], in_=gate[:, cols])

        transposes(0)
        copy_turned(0)
        quantise(0)
        fill()
        copy_bias(0, 0, True)
        copy_bias(0, 1, True)
        copy_bias(1, 0, True)

        def chunks_of(m):
            return STORE_CHUNKS if m >= ROW_TILES - 2 else 2

        for m in range(ROW_TILES):
            start_rows(m)
            ended = [group for group in GROUPS if group[-1] == m - 1]
            variance, power, factors = row_stats(ended[0]) if ended else ((), None, ())
            waits = bool(ended) and m - LAG in ended[0]
            evacuate(m, 0, variance[0:3])
            if m == 0:
                copy_bias(1, 1, True)
                copy_turned(1)
            if m + 1 < ROW_TILES and not waits:
                quantise(m + 1)
                fill()
            square(m, 0)
            if m + 2 < ROW_TILES:
                copy_turned(m + 2)
            evacuate(m, 1, (*variance[3:5], power) if ended else ())
            square(m, 1)
            if m + 1 < ROW_TILES and waits:
                quantise(m + 1)
                fill()
            if ended and not waits and m >= LAG:
                finish(m - LAG, chunks_of(m - LAG))
            for step in factors:
                step()
            if m >= LAG and (waits or not ended):
                finish(m - LAG, chunks_of(m - LAG))
        variance, power, factors = row_stats(GROUPS[-1])
        for i, m in enumerate(range(ROW_TILES - LAG, ROW_TILES)):
            finish(m, chunks_of(m))
            if i == 0:
                for step in variance:
                    step()
                power()
            if i == 1:
                for step in factors:
                    step()
